import numpy as np
import ml_dtypes


def mxq(x, axis, fmt="e4m3"):
    dtype, down = {"e4m3": (ml_dtypes.float8_e4m3fn, 7), "e5m2": (ml_dtypes.float8_e5m2, 14)}[fmt]
    v = np.moveaxis(np.asarray(x, np.float32).astype(ml_dtypes.bfloat16).astype(np.float64), axis, -1)
    blocks = v.reshape(v.shape[:-1] + (-1, 32))
    amax = np.abs(blocks).max(-1, keepdims=True)
    byte = np.maximum(np.where(amax > 0, np.frexp(amax)[1] - 1 + 127, 0) - down, 1)
    scale = np.exp2(byte - 127.0)
    codes = (blocks / scale).astype(np.float32).astype(dtype).astype(np.float64)
    return np.moveaxis((codes * scale).reshape(v.shape), -1, axis)


WIDE = False


def mx_kscale(k):
    if not WIDE:
        return np.ones(k)
    levels = np.array([10, -10, 5, -5, 0])
    a = np.random.permutation(np.resize(levels, k // 512 * 4)).reshape(k // 512, 4)
    idx = np.arange(k)
    return np.exp2(a[idx // 512, idx % 128 // 32])


BF16 = ml_dtypes.bfloat16


def bf(x):
    return np.asarray(x, np.float32).astype(BF16)


def f64(x):
    return np.asarray(x).astype(np.float64)


E2M1 = np.array([0.0, 0.5, 1.0, 1.5, 2.0, 3.0, 4.0, 6.0, -0.0, -0.5, -1.0, -1.5, -2.0, -3.0, -4.0, -6.0])


def pack_weight(w, fmt):
    k, n = w.shape
    w = f64(bf(w)).reshape(k // 32, 32, n)
    amax = np.abs(w).max(1)
    if fmt == "e4m3":
        byte = np.frexp(amax)[1] - 1 + 127 - 7
    else:
        mant, ex = np.frexp(amax / 6.0)
        byte = np.where(mant > 0.5, ex, ex - 1) + 127
    byte = np.clip(np.where(amax > 0, byte, 1), 1, 254)
    scaled = (w * np.exp2(127.0 - byte)[:, None, :]).reshape(k, n).astype(np.float32)
    by_word = np.ascontiguousarray(scaled.reshape(k // 512, 128, 4, n).transpose(0, 1, 3, 2))
    if fmt == "e4m3":
        words = by_word.astype(ml_dtypes.float8_e4m3fn).view(np.uint8)
    else:
        c = by_word.astype(ml_dtypes.float4_e2m1fn).view(np.uint8) & 0xF
        words = c[..., 0::2] | (c[..., 1::2] << 4)
    return np.ascontiguousarray(words), np.ascontiguousarray(byte.astype(np.uint8).reshape(k // 512, 16, n))


def unpack_weight(words, scales, fmt):
    g, p, n, _ = words.shape
    if fmt == "e4m3":
        vals = np.ascontiguousarray(words).view(ml_dtypes.float8_e4m3fn).astype(np.float64)
    else:
        nib = np.empty((g, p, n, 4), np.uint8)
        nib[..., 0::2] = words & 0xF
        nib[..., 1::2] = words >> 4
        vals = E2M1[nib]
    vals = vals * np.repeat(np.exp2(scales.astype(np.float64) - 127.0), 8, axis=1)[..., None]
    return vals.transpose(0, 1, 3, 2).reshape(g * 512, n)

def pack4(w):
    words, scales = pack_weight(w, "e2m1")
    return words.reshape(words.shape[0], 128, -1), scales


def unpack4(words, scales):
    return unpack_weight(words.reshape(words.shape[0], 128, -1, 2), scales, "e2m1")


B, C, P, NH, NW = 4, 4, 16, 16, 16
D = C * P * P
QK_SCALE = 1.0


def rel_bias(p):
    i = np.arange(p, dtype=np.float64)
    down = np.exp(-i / (p / 2))[:, None] * np.ones((1, p))
    right = down.T
    br = np.exp(-(i[:, None] + i[None, :]) / (p / 2))
    return np.stack([
        np.rot90(br, 2), np.flip(down, 0), np.rot90(br, 1),
        np.flip(right, 1), np.ones((p, p)), right,
        np.rot90(br, 3), down, br,
    ], axis=0)


def setup_inputs():
    s = mx_kscale(D)
    sx = np.tile(s.reshape(C, P, P), (1, NH, NW))
    x = bf(np.random.standard_normal((B, C, NH * P, NW * P)) * sx)
    w = np.random.standard_normal((3 * D, D)) / np.sqrt(D) / s
    words, scales = pack4(np.ascontiguousarray(w.T))
    b_qkv = bf(np.random.standard_normal(3 * D) * 0.5)
    return {"x": x,
            "W_qkv_words": words,
            "W_qkv_scales": scales,
            "b_qkv": b_qkv}


def reference(x, W_qkv_words, W_qkv_scales, b_qkv):
    p, c = P, C
    b, _, h, w = x.shape
    nh, nw = h // p, w // p
    feat = f64(x).reshape(b, c, nh, p, nw, p).transpose(0, 2, 4, 1, 3, 5).reshape(b, nh, nw, c * p * p)
    y = mxq(feat, 3, "e4m3") @ unpack4(W_qkv_words, W_qkv_scales)
    qkv = np.pad(y, ((0, 0), (1, 1), (1, 1), (0, 0))) + f64(b_qkv)
    qkv = qkv.reshape(b, nh + 2, nw + 2, 3, c, p, p)
    core_q = qkv[:, 1:nh + 1, 1:nw + 1, 0] * QK_SCALE
    k = np.stack([qkv[:, di:di + nh, dj:dj + nw, 1] for di in range(3) for dj in range(3)], axis=3)
    v = np.stack([qkv[:, di:di + nh, dj:dj + nw, 2] for di in range(3) for dj in range(3)], axis=3)
    bias = rel_bias(p)
    attn = core_q[:, :, :, None] * k * bias[:, None]
    out = np.sum(attn * v, axis=3)
    return out.transpose(0, 3, 1, 4, 2, 5).reshape(b, c, nh * p, nw * p)

@@ -1,0 +1,248 @@
+from contextlib import ExitStack
+
+import concourse.mybir as mybir
+from concourse.masks import make_identity
+
+F32 = mybir.dt.float32
+BF16 = mybir.dt.bfloat16
+I32 = mybir.dt.int32
+U32 = mybir.dt.uint32
+U8 = mybir.dt.uint8
+FP8X4 = mybir.dt.float8_e4m3fn_x4
+FP4X4 = mybir.dt.float4_e2m1fn_x4
+ALU = mybir.AluOpType
+ACT = mybir.ActivationFunctionType
+
+P = 128
+GRID = 16
+PATCH = 16
+CHANNELS = 4
+D = CHANNELS * PATCH * PATCH
+PASSES = 2
+HALVES = 2
+PAIR = 2
+COLS = GRID * GRID * PAIR
+ROW_HALVES = 2
+ROWS = PATCH // ROW_HALVES
+TILES = D // P
+Q = 0
+K = 1
+V = 2
+PER_BANK = 4
+
+PREV_S = 0
+NEXT_S = 1
+PREV_R = 2
+NEXT_R = 4
+
+FLOPS = 2 * 4 * GRID * GRID * D * 3 * D
+
+
+def tile_attentionconv_kernel(tc, x, W_qkv_words, W_qkv_scales, b_qkv, out):
+    nc = tc.nc
+    with ExitStack() as ctx:
+        ctx.enter_context(tc.manual_schedule())
+        consts = ctx.enter_context(tc.tile_pool(name="consts", bufs=1))
+        operands = ctx.enter_context(tc.tile_pool(name="operands", bufs=1))
+        work = ctx.enter_context(tc.tile_pool(name="work", bufs=2))
+        psum = ctx.enter_context(tc.psum_pool(name="psum", bufs=8))
+
+        b_rows = consts.tile([P, P], BF16, name="b_rows")
+        nc.vector.memset(b_rows[:], 0.0)
+        nc.scalar.dma_start(out=b_rows[0 : 3 * TILES, :], in_=b_qkv.rearrange("(t p) -> t p", p=P))
+
+        x_nat = operands.tile([P, 2, PATCH * GRID * PATCH], BF16, name="x_nat")
+        x_rows = x.rearrange("b (g c) (i r) w -> c i b g (r w)", g=PASSES, c=2, i=GRID, r=PATCH)
+        for c in range(2):
+            nc.sync.dma_start(out=x_nat[:, c, :], in_=x_rows[c])
+
+        w_scales = operands.tile([P, PASSES, 3 * D], U8, name="w_scales", align_bytes=64)
+        nc.vector.memset(w_scales[:].bitcast(I32), 0)
+        for quadrant in range(4):
+            nc.sync.dma_start(
+                out=w_scales[32 * quadrant : 32 * quadrant + 4, :, :].bitcast(I32),
+                in_=W_qkv_scales[:, 4 * quadrant : 4 * quadrant + 4, :].rearrange("g r n -> r g n").bitcast(I32),
+            )
+        w_words = operands.tile([P, PASSES, 2 * 3 * D], U8, name="w_words", align_bytes=64)
+        for proj in (K, V, Q):
+            for g in range(PASSES):
+                cols = slice(2 * D * proj, 2 * D * (proj + 1))
+                nc.sync.dma_start(out=w_words[:, g, cols].bitcast(I32), in_=W_qkv_words[g, :, cols].bitcast(I32))
+
+        ident = consts.tile([P, P], F32, name="ident")
+        part_idx = consts.tile([P, 1], I32, name="part_idx")
+        nc.gpsimd.iota(part_idx[:], pattern=[[0, 1]], base=0, channel_multiplier=1)
+        make_identity(nc, ident[:])
+
+        s_int = consts.tile([P, 1], I32, name="s_int")
+        r_int = consts.tile([P, 1], I32, name="r_int")
+        nc.vector.tensor_single_scalar(out=s_int[:], in_=part_idx[:], scalar=PATCH - 1, op=ALU.bitwise_and)
+        nc.vector.tensor_single_scalar(out=r_int[:], in_=part_idx[:], scalar=4, op=ALU.arith_shift_right)
+        s_pos = consts.tile([P, 1], F32, name="s_pos")
+        r_pos = consts.tile([P, 1], F32, name="r_pos")
+        nc.vector.tensor_copy(out=s_pos[:], in_=s_int[:])
+        nc.vector.tensor_copy(out=r_pos[:], in_=r_int[:])
+
+        exponents = consts.tile([P, 6], F32, name="exponents")
+
+        def exponent(col, pos, sign, offset):
+            nc.vector.tensor_scalar(
+                out=exponents[:, col : col + 1], in0=pos[:], scalar1=sign, scalar2=offset, op0=ALU.mult, op1=ALU.add
+            )
+
+        exponent(PREV_S, s_pos, 1.0, -15.0)
+        exponent(NEXT_S, s_pos, -1.0, 0.0)
+        for rh in range(ROW_HALVES):
+            exponent(PREV_R + rh, r_pos, 1.0, ROWS * rh - 15.0)
+            exponent(NEXT_R + rh, r_pos, -1.0, -1.0 * ROWS * rh)
+        factors = consts.tile([P, 6], F32, name="factors")
+        nc.scalar.activation(out=factors[:], in_=exponents[:], func=ACT.Exp, scale=1.0 / 8.0)
+
+        def factor(col):
+            return factors[:, col : col + 1]
+
+        b_square = consts.tile([P, P], F32, name="b_square")
+        nc.vector.tensor_copy(out=b_square[:], in_=b_rows[:])
+        b_turned = psum.tile([P, P], F32, name="b_turned", tag="bank")
+        nc.tensor.transpose(b_turned[:], b_square[:], ident[:])
+        bias = consts.tile([P, 3 * TILES], F32, name="bias")
+        nc.vector.tensor_copy(out=bias[:], in_=b_turned[:, 0 : 3 * TILES])
+
+        def bias_of(proj, ch, rh):
+            col = proj * TILES + ch * ROW_HALVES + rh
+            return bias[:, col : col + 1]
+
+        kv_outside = consts.tile([P, TILES], F32, name="kv_outside")
+        nc.vector.tensor_mul(out=kv_outside[:], in0=bias[:, K * TILES : (K + 1) * TILES], in1=bias[:, V * TILES : (V + 1) * TILES])
+        side_factors = consts.tile([P, 1], F32, name="side_factors")
+        nc.vector.tensor_add(out=side_factors[:], in0=factor(PREV_S), in1=factor(NEXT_S))
+        row_outside = consts.tile([P, TILES], F32, name="row_outside")
+        nc.vector.scalar_tensor_tensor(
+            out=row_outside[:], in0=kv_outside[:], scalar=side_factors[:], in1=kv_outside[:], op0=ALU.mult, op1=ALU.add
+        )
+
+        zeros = consts.tile([P, 2 * GRID * PAIR], F32, name="zeros")
+        nc.vector.memset(zeros[:], 0.0)
+        kv = []
+        row_sum = []
+        for rh in range(ROW_HALVES):
+            kv.append(consts.tile([P, GRID + 2, CHANNELS, GRID, PAIR], F32, name="kv%d" % rh))
+            row_sum.append(consts.tile([P, GRID, CHANNELS, GRID + 2, PAIR], F32, name="row_sum%d" % rh))
+            for ch in range(CHANNELS):
+                tile_col = ch * ROW_HALVES + rh
+                nc.scalar.activation(
+                    out=kv[rh][:, 0 : GRID + 2 : GRID + 1, ch, :, :],
+                    in_=zeros[:].rearrange("p (a i e) -> p a i e", a=2, e=PAIR),
+                    func=ACT.Identity,
+                    bias=kv_outside[:, tile_col : tile_col + 1],
+                )
+                nc.vector.tensor_scalar_add(
+                    out=row_sum[rh][:, :, ch, 0 : GRID + 2 : GRID + 1, :],
+                    in0=zeros[:].rearrange("p (j a e) -> p j a e", a=2, e=PAIR),
+                    scalar1=row_outside[:, tile_col : tile_col + 1],
+                )
+
+        x_words = x_nat[:].bitcast(F32).rearrange("p c (r j q u) -> p c u j r q", r=PATCH, j=GRID, q=4, u=2)
+        x_sorted = operands.tile([P, GRID, 2, P], F32, name="x_sorted")
+        x_sorted_view = x_sorted[:].rearrange("p j u (c r q) -> p c u j r q", c=2, r=PATCH, q=4)
+        for c in range(2):
+            for u in range(2):
+                nc.vector.tensor_copy(out=x_sorted_view[:, c, u], in_=x_words[:, c, u])
+
+        x_grouped = operands.tile([P, HALVES * PASSES, 4 * COLS], BF16, name="x_grouped", align_bytes=64)
+        x_grouped_words = x_grouped[:].bitcast(F32).rearrange("p n (j m u) -> p n j m u", j=GRID, u=2)
+        for bank in range(GRID // 2):
+            x_turned = psum.tile([P, 2, 2, P], F32, name="x_turned", tag="bank")
+            for jj in range(2):
+                for u in range(2):
+                    nc.tensor.transpose(x_turned[:, jj, u, :], x_sorted[:, 2 * bank + jj, u, :], ident[:])
+            copy_out = nc.vector.tensor_copy if bank % 2 == 0 else nc.scalar.copy
+            for jj in range(2):
+                copy_out(
+                    out=x_grouped_words[:, :, 2 * bank + jj, :, :],
+                    in_=x_turned[:, jj].rearrange("p u (m n) -> p n m u", n=HALVES * PASSES),
+                )
+
+        x_codes = operands.tile([P, HALVES * PASSES, COLS], U32, name="x_codes", align_bytes=64)
+        x_scales = operands.tile([P, HALVES * PASSES, COLS], U8, name="x_scales", align_bytes=64)
+        for n in range(HALVES * PASSES):
+            nc.vector.quantize_mx(out=x_codes[:, n, :].bitcast(FP8X4), scales=x_scales[:, n, :], in_=x_grouped[:, n, :])
+
+        def project(proj, half, ch, rh):
+            first = proj * D + (ch * ROW_HALVES + rh) * P
+            acc = psum.tile([P, COLS], F32, name="acc", tag="bank")
+            for g in range(PASSES):
+                nc.tensor.matmul_mx(
+                    out=acc[:],
+                    lhsT=w_words[:, g, 2 * first : 2 * (first + P)].bitcast(FP4X4),
+                    lhsT_scale=w_scales[:, g, first : first + P],
+                    rhs=x_codes[:, half * PASSES + g, :].bitcast(FP8X4),
+                    rhs_scale=x_scales[:, half * PASSES + g, :],
+                    start=(g == 0),
+                    stop=(g == PASSES - 1),
+                )
+            return acc[:].rearrange("p (j i e) -> p j i e", j=GRID, e=PAIR)
+
+        def keys_times_values(half, rh):
+            for ch in range(CHANNELS):
+                k_acc = project(K, half, ch, rh)
+                v_acc = project(V, half, ch, rh)
+                k_sb = work.tile([P, GRID, GRID, PAIR], F32, name="k_sb", bufs=CHANNELS)
+                nc.scalar.activation(out=k_sb[:], in_=k_acc, func=ACT.Identity, bias=bias_of(K, ch, rh))
+                nc.vector.scalar_tensor_tensor(
+                    out=kv[rh][:, 1 : GRID + 1, ch, :, :],
+                    in0=v_acc,
+                    scalar=bias_of(V, ch, rh),
+                    in1=k_sb[:],
+                    op0=ALU.add,
+                    op1=ALU.mult,
+                )
+
+        def queries(half, rh):
+            q_sb = work.tile([P, GRID, CHANNELS, GRID, PAIR], F32, name="q_sb")
+            for ch in range(CHANNELS):
+                q_acc = project(Q, half, ch, rh)
+                nc.scalar.activation(out=q_sb[:, :, ch, :, :], in_=q_acc, func=ACT.Identity, bias=bias_of(Q, ch, rh))
+            return q_sb
+
+        def weigh_neighbours(rh, q_sb):
+            def add_scaled(out_, shifted, col, onto):
+                nc.vector.scalar_tensor_tensor(
+                    out=out_, in0=shifted, scalar=factor(col), in1=onto, op0=ALU.mult, op1=ALU.add
+                )
+
+            inner = row_sum[rh][:, :, :, 1 : GRID + 1, :]
+            add_scaled(inner, kv[rh][:, 0:GRID], PREV_S, kv[rh][:, 1 : GRID + 1])
+            add_scaled(inner, kv[rh][:, 2 : GRID + 2], NEXT_S, inner)
+            result = work.tile([P, GRID, CHANNELS, GRID, PAIR], F32, name="result")
+            add_scaled(result[:], row_sum[rh][:, :, :, 0:GRID, :], PREV_R + rh, inner)
+            add_scaled(result[:], row_sum[rh][:, :, :, 2 : GRID + 2, :], NEXT_R + rh, result[:])
+            nc.vector.tensor_mul(out=result[:], in0=q_sb[:], in1=result[:])
+            return result
+
+        out_rows = out.rearrange(
+            "(e h) c (i a l) w -> h a c i e (l w)", e=PAIR, h=HALVES, i=GRID, a=ROW_HALVES, l=ROWS
+        )
+
+        def write_out(half, rh, result):
+            pixels = work.tile([P, ROWS, GRID, PATCH], F32, name="pixels")
+            for bank in range(GRID // PER_BANK):
+                turned = psum.tile([P, PER_BANK, P], F32, name="turned", tag="bank")
+                for jj in range(PER_BANK):
+                    columns = result[:, bank * PER_BANK + jj].rearrange("p c i e -> p (c i e)")
+                    nc.tensor.transpose(turned[:, jj, :], columns, ident[:])
+                nc.scalar.copy(
+                    out=pixels[:, :, bank * PER_BANK : (bank + 1) * PER_BANK, :],
+                    in_=turned[:].rearrange("p j (l s) -> p l j s", l=ROWS),
+                )
+            nc.sync.dma_start(out=out_rows[half][rh], in_=pixels[:].rearrange("p l j s -> p (l j s)"))
+
+        waiting = None
+        for half in range(HALVES):
+            for rh in range(ROW_HALVES):
+                keys_times_values(half, rh)
+                if waiting is not None:
+                    write_out(*waiting)
+                q_sb = queries(half, rh)
+                waiting = (half, rh, weigh_neighbours(rh, q_sb))
+        write_out(*waiting)

@@ -101,6 +101,16 @@ def tile_attentionconv_kernel(tc, x, W_qkv_words, W_qkv_scales, b_qkv, out):
         def factor(col):
             return factors[:, col : col + 1]
 
+        x_words = x_nat[:].bitcast(F32).rearrange("p c (r j q u) -> p c u j r q", r=PATCH, j=GRID, q=4, u=2)
+        x_sorted = operands.tile([P, GRID, 2, P], F32, name="x_sorted")
+        x_sorted_view = x_sorted[:].rearrange("p j u (c r q) -> p c u j r q", c=2, r=PATCH, q=4)
+
+        def sort_words(c):
+            for u in range(2):
+                nc.vector.tensor_copy(out=x_sorted_view[:, c, u], in_=x_words[:, c, u])
+
+        sort_words(0)
+
         b_square = consts.tile([P, P], F32, name="b_square")
         nc.vector.tensor_copy(out=b_square[:], in_=b_rows[:])
         b_turned = psum.tile([P, P], F32, name="b_turned", tag="bank")
@@ -142,12 +152,7 @@ def tile_attentionconv_kernel(tc, x, W_qkv_words, W_qkv_scales, b_qkv, out):
                     scalar1=row_outside[:, tile_col : tile_col + 1],
                 )
 
-        x_words = x_nat[:].bitcast(F32).rearrange("p c (r j q u) -> p c u j r q", r=PATCH, j=GRID, q=4, u=2)
-        x_sorted = operands.tile([P, GRID, 2, P], F32, name="x_sorted")
-        x_sorted_view = x_sorted[:].rearrange("p j u (c r q) -> p c u j r q", c=2, r=PATCH, q=4)
-        for c in range(2):
-            for u in range(2):
-                nc.vector.tensor_copy(out=x_sorted_view[:, c, u], in_=x_words[:, c, u])
+        sort_words(1)
 
         x_grouped = operands.tile([P, HALVES * PASSES, 4 * COLS], BF16, name="x_grouped", align_bytes=64)
         x_grouped_words = x_grouped[:].bitcast(F32).rearrange("p n (j m u) -> p n j m u", j=GRID, u=2)
@@ -211,17 +216,27 @@ def tile_attentionconv_kernel(tc, x, W_qkv_words, W_qkv_scales, b_qkv, out):
                     out=out_, in0=shifted, scalar=factor(col), in1=onto, op0=ALU.mult, op1=ALU.add
                 )
 
-            inner = row_sum[rh][:, :, :, 1 : GRID + 1, :]
-            add_scaled(inner, kv[rh][:, 0:GRID], PREV_S, kv[rh][:, 1 : GRID + 1])
-            add_scaled(inner, kv[rh][:, 2 : GRID + 2], NEXT_S, inner)
+            products = kv[rh]
+            sums = row_sum[rh]
             result = work.tile([P, GRID, CHANNELS, GRID, PAIR], F32, name="result")
-            add_scaled(result[:], row_sum[rh][:, :, :, 0:GRID, :], PREV_R + rh, inner)
-            add_scaled(result[:], row_sum[rh][:, :, :, 2 : GRID + 2, :], NEXT_R + rh, result[:])
-            nc.vector.tensor_mul(out=result[:], in0=q_sb[:], in1=result[:])
+            halves_of_j = ((0, GRID // 2), (GRID // 2, GRID))
+            for j0, j1 in halves_of_j:
+                add_scaled(sums[:, j0:j1, :, 1 : GRID + 1, :], products[:, j0:j1], PREV_S, products[:, j0 + 1 : j1 + 1])
+            for j0, j1 in halves_of_j:
+                inner = sums[:, j0:j1, :, 1 : GRID + 1, :]
+                add_scaled(inner, products[:, j0 + 2 : j1 + 2], NEXT_S, inner)
+            for j0, j1 in halves_of_j:
+                add_scaled(result[:, j0:j1], sums[:, j0:j1, :, 0:GRID, :], PREV_R + rh, sums[:, j0:j1, :, 1 : GRID + 1, :])
+            for j0, j1 in halves_of_j:
+                add_scaled(result[:, j0:j1], sums[:, j0:j1, :, 2 : GRID + 2, :], NEXT_R + rh, result[:, j0:j1])
+            for j0 in range(0, GRID, PER_BANK):
+                nc.vector.tensor_mul(
+                    out=result[:, j0 : j0 + PER_BANK], in0=q_sb[:, j0 : j0 + PER_BANK], in1=result[:, j0 : j0 + PER_BANK]
+                )
             return result
 
         out_rows = out.rearrange(
-            "(e h) c (i a l) w -> h a c i e (l w)", e=PAIR, h=HALVES, i=GRID, a=ROW_HALVES, l=ROWS
+            "(e h) c (i a l) (j s) -> h a e (c i) l j s", e=PAIR, h=HALVES, i=GRID, a=ROW_HALVES, l=ROWS, s=PATCH
         )
 
         def write_out(half, rh, result):
@@ -231,11 +246,10 @@ def tile_attentionconv_kernel(tc, x, W_qkv_words, W_qkv_scales, b_qkv, out):
                 for jj in range(PER_BANK):
                     columns = result[:, bank * PER_BANK + jj].rearrange("p c i e -> p (c i e)")
                     nc.tensor.transpose(turned[:, jj, :], columns, ident[:])
-                nc.scalar.copy(
-                    out=pixels[:, :, bank * PER_BANK : (bank + 1) * PER_BANK, :],
-                    in_=turned[:].rearrange("p j (l s) -> p l j s", l=ROWS),
-                )
-            nc.sync.dma_start(out=out_rows[half][rh], in_=pixels[:].rearrange("p l j s -> p (l j s)"))
+                js = slice(bank * PER_BANK, (bank + 1) * PER_BANK)
+                nc.scalar.copy(out=pixels[:, :, js, :], in_=turned[:].rearrange("p j (l s) -> p l j s", l=ROWS))
+                for pair in range(PAIR):
+                    nc.sync.dma_start(out=out_rows[half][rh][pair][:, :, js, :], in_=pixels[pair:P:PAIR, :, js, :])
 
         waiting = None
         for half in range(HALVES):

@@ -124,32 +124,40 @@ def tile_attentionconv_kernel(tc, x, W_qkv_words, W_qkv_scales, b_qkv, out):
 
         kv_outside = consts.tile([P, TILES], F32, name="kv_outside")
         nc.vector.tensor_mul(out=kv_outside[:], in0=bias[:, K * TILES : (K + 1) * TILES], in1=bias[:, V * TILES : (V + 1) * TILES])
-        side_factors = consts.tile([P, 1], F32, name="side_factors")
-        nc.vector.tensor_add(out=side_factors[:], in0=factor(PREV_S), in1=factor(NEXT_S))
-        row_outside = consts.tile([P, TILES], F32, name="row_outside")
-        nc.vector.scalar_tensor_tensor(
-            out=row_outside[:], in0=kv_outside[:], scalar=side_factors[:], in1=kv_outside[:], op0=ALU.mult, op1=ALU.add
-        )
+        col_outside = consts.tile([P, TILES], F32, name="col_outside")
+        for rh in range(ROW_HALVES):
+            r_factors = consts.tile([P, 1], F32, name="r_factors%d" % rh)
+            nc.vector.tensor_add(out=r_factors[:], in0=factor(PREV_R + rh), in1=factor(NEXT_R + rh))
+            of_rh = slice(rh, TILES, ROW_HALVES)
+            nc.vector.scalar_tensor_tensor(
+                out=col_outside[:, of_rh], in0=kv_outside[:, of_rh], scalar=r_factors[:], in1=kv_outside[:, of_rh],
+                op0=ALU.mult, op1=ALU.add,
+            )
+        left_outside = consts.tile([P, TILES], F32, name="left_outside")
+        right_outside = consts.tile([P, TILES], F32, name="right_outside")
+        nc.vector.tensor_scalar_mul(out=left_outside[:], in0=col_outside[:], scalar1=factor(PREV_S))
+        nc.vector.tensor_scalar_mul(out=right_outside[:], in0=col_outside[:], scalar1=factor(NEXT_S))
 
         zeros = consts.tile([P, 2 * GRID * PAIR], F32, name="zeros")
         nc.vector.memset(zeros[:], 0.0)
         kv = []
-        row_sum = []
+        left = []
+        right = []
         for rh in range(ROW_HALVES):
-            kv.append(consts.tile([P, GRID + 2, CHANNELS, GRID, PAIR], F32, name="kv%d" % rh))
-            row_sum.append(consts.tile([P, GRID, CHANNELS, GRID + 2, PAIR], F32, name="row_sum%d" % rh))
+            kv.append(consts.tile([P, GRID, CHANNELS, GRID + 2, PAIR], F32, name="kv%d" % rh))
+            left.append(consts.tile([P, GRID, CHANNELS, GRID, PAIR], F32, name="left%d" % rh))
+            right.append(consts.tile([P, GRID, CHANNELS, GRID, PAIR], F32, name="right%d" % rh))
             for ch in range(CHANNELS):
-                tile_col = ch * ROW_HALVES + rh
-                nc.scalar.activation(
-                    out=kv[rh][:, 0 : GRID + 2 : GRID + 1, ch, :, :],
-                    in_=zeros[:].rearrange("p (a i e) -> p a i e", a=2, e=PAIR),
-                    func=ACT.Identity,
-                    bias=kv_outside[:, tile_col : tile_col + 1],
-                )
+                tile_col = slice(ch * ROW_HALVES + rh, ch * ROW_HALVES + rh + 1)
                 nc.vector.tensor_scalar_add(
-                    out=row_sum[rh][:, :, ch, 0 : GRID + 2 : GRID + 1, :],
+                    out=kv[rh][:, :, ch, 0 : GRID + 2 : GRID + 1, :],
                     in0=zeros[:].rearrange("p (j a e) -> p j a e", a=2, e=PAIR),
-                    scalar1=row_outside[:, tile_col : tile_col + 1],
+                    scalar1=kv_outside[:, tile_col],
+                )
+                one_column = zeros[:, 0 : GRID * PAIR].rearrange("p (i e) -> p i e", e=PAIR)
+                nc.scalar.activation(out=left[rh][:, 0, ch], in_=one_column, func=ACT.Identity, bias=left_outside[:, tile_col])
+                nc.scalar.activation(
+                    out=right[rh][:, GRID - 1, ch], in_=one_column, func=ACT.Identity, bias=right_outside[:, tile_col]
                 )
 
         sort_words(1)
@@ -195,7 +203,7 @@ def tile_attentionconv_kernel(tc, x, W_qkv_words, W_qkv_scales, b_qkv, out):
                 k_sb = work.tile([P, GRID, GRID, PAIR], F32, name="k_sb", bufs=CHANNELS)
                 nc.scalar.activation(out=k_sb[:], in_=k_acc, func=ACT.Identity, bias=bias_of(K, ch, rh))
                 nc.vector.scalar_tensor_tensor(
-                    out=kv[rh][:, 1 : GRID + 1, ch, :, :],
+                    out=kv[rh][:, :, ch, 1 : GRID + 1, :],
                     in0=v_acc,
                     scalar=bias_of(V, ch, rh),
                     in1=k_sb[:],
@@ -210,44 +218,58 @@ def tile_attentionconv_kernel(tc, x, W_qkv_words, W_qkv_scales, b_qkv, out):
                 nc.scalar.activation(out=q_sb[:, :, ch, :, :], in_=q_acc, func=ACT.Identity, bias=bias_of(Q, ch, rh))
             return q_sb
 
-        def weigh_neighbours(rh, q_sb):
-            def add_scaled(out_, shifted, col, onto):
-                nc.vector.scalar_tensor_tensor(
-                    out=out_, in0=shifted, scalar=factor(col), in1=onto, op0=ALU.mult, op1=ALU.add
-                )
+        halves_of_j = ((0, GRID // 2), (GRID // 2, GRID))
 
-            products = kv[rh]
-            sums = row_sum[rh]
-            result = work.tile([P, GRID, CHANNELS, GRID, PAIR], F32, name="result")
-            halves_of_j = ((0, GRID // 2), (GRID // 2, GRID))
+        def sum_columns(rh):
+            col_sum = work.tile([P, GRID, CHANNELS, GRID, PAIR], F32, name="col_sum")
             for j0, j1 in halves_of_j:
-                add_scaled(sums[:, j0:j1, :, 1 : GRID + 1, :], products[:, j0:j1], PREV_S, products[:, j0 + 1 : j1 + 1])
-            for j0, j1 in halves_of_j:
-                inner = sums[:, j0:j1, :, 1 : GRID + 1, :]
-                add_scaled(inner, products[:, j0 + 2 : j1 + 2], NEXT_S, inner)
-            for j0, j1 in halves_of_j:
-                add_scaled(result[:, j0:j1], sums[:, j0:j1, :, 0:GRID, :], PREV_R + rh, sums[:, j0:j1, :, 1 : GRID + 1, :])
-            for j0, j1 in halves_of_j:
-                add_scaled(result[:, j0:j1], sums[:, j0:j1, :, 2 : GRID + 2, :], NEXT_R + rh, result[:, j0:j1])
-            for j0 in range(0, GRID, PER_BANK):
-                nc.vector.tensor_mul(
-                    out=result[:, j0 : j0 + PER_BANK], in0=q_sb[:, j0 : j0 + PER_BANK], in1=result[:, j0 : j0 + PER_BANK]
+                nc.vector.scalar_tensor_tensor(
+                    out=col_sum[:, j0:j1], in0=kv[rh][:, j0:j1, :, 0:GRID, :], scalar=factor(PREV_R + rh),
+                    in1=kv[rh][:, j0:j1, :, 1 : GRID + 1, :], op0=ALU.mult, op1=ALU.add,
                 )
-            return result
+            for j0, j1 in halves_of_j:
+                nc.vector.scalar_tensor_tensor(
+                    out=col_sum[:, j0:j1], in0=kv[rh][:, j0:j1, :, 2 : GRID + 2, :], scalar=factor(NEXT_R + rh),
+                    in1=col_sum[:, j0:j1], op0=ALU.mult, op1=ALU.add,
+                )
+            for j0, j1 in halves_of_j:
+                nc.gpsimd.tensor_scalar(
+                    out=left[rh][:, max(j0, 1) : j1], in0=col_sum[:, max(j0, 1) - 1 : j1 - 1],
+                    scalar1=factor(PREV_S), scalar2=0.0, op0=ALU.mult, op1=ALU.add,
+                )
+                nc.gpsimd.tensor_scalar(
+                    out=right[rh][:, j0 : min(j1, GRID - 1)], in0=col_sum[:, j0 + 1 : min(j1, GRID - 1) + 1],
+                    scalar1=factor(NEXT_S), scalar2=0.0, op0=ALU.mult, op1=ALU.add,
+                )
+            return col_sum
 
         out_rows = out.rearrange(
             "(e h) c (i a l) (j s) -> h a e (c i) l j s", e=PAIR, h=HALVES, i=GRID, a=ROW_HALVES, l=ROWS, s=PATCH
         )
 
-        def write_out(half, rh, result):
+        def columns_of(group_tile, j):
+            return group_tile[:, j].rearrange("p c i e -> p (c i e)")
+
+        def by_pixel_row(turned):
+            return turned[:].rearrange("p j (l s) -> p l j s", l=ROWS)
+
+        def finish(half, rh, q_sb, col_sum):
             pixels = work.tile([P, ROWS, GRID, PATCH], F32, name="pixels")
             for bank in range(GRID // PER_BANK):
-                turned = psum.tile([P, PER_BANK, P], F32, name="turned", tag="bank")
-                for jj in range(PER_BANK):
-                    columns = result[:, bank * PER_BANK + jj].rearrange("p c i e -> p (c i e)")
-                    nc.tensor.transpose(turned[:, jj, :], columns, ident[:])
                 js = slice(bank * PER_BANK, (bank + 1) * PER_BANK)
-                nc.scalar.copy(out=pixels[:, :, js, :], in_=turned[:].rearrange("p j (l s) -> p l j s", l=ROWS))
+                q_turned = psum.tile([P, PER_BANK, P], F32, name="q_turned", tag="bank")
+                sum_turned = psum.tile([P, PER_BANK, P], F32, name="sum_turned", tag="bank")
+                for jj in range(PER_BANK):
+                    nc.tensor.transpose(q_turned[:, jj, :], columns_of(q_sb, bank * PER_BANK + jj), ident[:])
+                for jj in range(PER_BANK):
+                    terms = (col_sum, left[rh], right[rh])
+                    for n, term in enumerate(terms):
+                        nc.tensor.matmul(
+                            sum_turned[:, jj, :], lhsT=columns_of(term, bank * PER_BANK + jj), rhs=ident[:],
+                            is_transpose=True, start=(n == 0), stop=(n == len(terms) - 1),
+                        )
+                nc.scalar.copy(out=pixels[:, :, js, :], in_=by_pixel_row(q_turned))
+                nc.vector.tensor_mul(out=pixels[:, :, js, :], in0=by_pixel_row(sum_turned), in1=pixels[:, :, js, :])
                 for pair in range(PAIR):
                     nc.sync.dma_start(out=out_rows[half][rh][pair][:, :, js, :], in_=pixels[pair:P:PAIR, :, js, :])
 
@@ -255,8 +277,8 @@ def tile_attentionconv_kernel(tc, x, W_qkv_words, W_qkv_scales, b_qkv, out):
         for half in range(HALVES):
             for rh in range(ROW_HALVES):
                 keys_times_values(half, rh)
+                col_sum = sum_columns(rh)
                 if waiting is not None:
-                    write_out(*waiting)
-                q_sb = queries(half, rh)
-                waiting = (half, rh, weigh_neighbours(rh, q_sb))
-        write_out(*waiting)
+                    finish(*waiting)
+                waiting = (half, rh, queries(half, rh), col_sum)
+        finish(*waiting)

@@ -35,6 +35,9 @@ NEXT_S = 1
 PREV_R = 2
 NEXT_R = 4
 
+WARM_PER_PART = 3
+WARM_AFTER = 5
+
 FLOPS = 2 * 4 * GRID * GRID * D * 3 * D
 
 
@@ -49,12 +52,16 @@ def tile_attentionconv_kernel(tc, x, W_qkv_words, W_qkv_scales, b_qkv, out):
 
         b_rows = consts.tile([P, P], BF16, name="b_rows")
         nc.vector.memset(b_rows[:], 0.0)
-        nc.scalar.dma_start(out=b_rows[0 : 3 * TILES, :], in_=b_qkv.rearrange("(t p) -> t p", p=P))
+        b_tiles = b_qkv.rearrange("(t p) -> t p", p=P)
+        for rows in (slice(0, 2 * TILES), slice(2 * TILES, 3 * TILES)):
+            nc.sync.dma_start(out=b_rows[rows, :], in_=b_tiles[rows, :])
 
-        x_nat = operands.tile([P, 2, PATCH * GRID * PATCH], BF16, name="x_nat")
-        x_rows = x.rearrange("b (g c) (i r) w -> c i b g (r w)", g=PASSES, c=2, i=GRID, r=PATCH)
-        for c in range(2):
-            nc.sync.dma_start(out=x_nat[:, c, :], in_=x_rows[c])
+        x_rows = x.rearrange("b (g c) (i h r) w -> c h i b g (r w)", g=PASSES, c=2, i=GRID, h=ROW_HALVES, r=ROWS)
+        parts = [(c, h) for c in range(2) for h in range(ROW_HALVES)]
+        x_nat = {}
+        for c, h in parts:
+            x_nat[c, h] = operands.tile([P, ROWS * GRID * PATCH], BF16, name="x_nat%d%d" % (c, h))
+            nc.sync.dma_start(out=x_nat[c, h][:], in_=x_rows[c][h])
 
         w_scales = operands.tile([P, PASSES, 3 * D], U8, name="w_scales", align_bytes=64)
         nc.vector.memset(w_scales[:].bitcast(I32), 0)
@@ -73,6 +80,8 @@ def tile_attentionconv_kernel(tc, x, W_qkv_words, W_qkv_scales, b_qkv, out):
         part_idx = consts.tile([P, 1], I32, name="part_idx")
         nc.gpsimd.iota(part_idx[:], pattern=[[0, 1]], base=0, channel_multiplier=1)
         make_identity(nc, ident[:])
+        idle_w = consts.tile([P, P], BF16, name="idle_w")
+        nc.gpsimd.memset(idle_w[:], 0.0)
 
         s_int = consts.tile([P, 1], I32, name="s_int")
         r_int = consts.tile([P, 1], I32, name="r_int")
@@ -101,15 +110,8 @@ def tile_attentionconv_kernel(tc, x, W_qkv_words, W_qkv_scales, b_qkv, out):
         def factor(col):
             return factors[:, col : col + 1]
 
-        x_words = x_nat[:].bitcast(F32).rearrange("p c (r j q u) -> p c u j r q", r=PATCH, j=GRID, q=4, u=2)
-        x_sorted = operands.tile([P, GRID, 2, P], F32, name="x_sorted")
-        x_sorted_view = x_sorted[:].rearrange("p j u (c r q) -> p c u j r q", c=2, r=PATCH, q=4)
-
-        def sort_words(c):
-            for u in range(2):
-                nc.vector.tensor_copy(out=x_sorted_view[:, c, u], in_=x_words[:, c, u])
-
-        sort_words(0)
+        zeros = consts.tile([P, 2 * GRID * PAIR], F32, name="zeros")
+        nc.vector.memset(zeros[:], 0.0)
 
         b_square = consts.tile([P, P], F32, name="b_square")
         nc.vector.tensor_copy(out=b_square[:], in_=b_rows[:])
@@ -138,8 +140,57 @@ def tile_attentionconv_kernel(tc, x, W_qkv_words, W_qkv_scales, b_qkv, out):
         nc.vector.tensor_scalar_mul(out=left_outside[:], in0=col_outside[:], scalar1=factor(PREV_S))
         nc.vector.tensor_scalar_mul(out=right_outside[:], in0=col_outside[:], scalar1=factor(NEXT_S))
 
-        zeros = consts.tile([P, 2 * GRID * PAIR], F32, name="zeros")
-        nc.vector.memset(zeros[:], 0.0)
+        x_sorted = [operands.tile([P, GRID, P], F32, name="x_sorted%d" % u) for u in range(2)]
+        sorters = (nc.vector.tensor_copy, nc.scalar.copy)
+
+        def keep_clock(product, part, times):
+            for n in range(times):
+                nc.tensor.matmul(product[:], lhsT=idle_w[:], rhs=x_nat[part][:, 0:COLS], start=True, stop=True)
+
+        unread = psum.tile([P, COLS], F32, name="unread", tag="bank")
+        for part in parts:
+            c, h = part
+            words = x_nat[part][:].bitcast(F32).rearrange("p (r j q u) -> p u j r q", r=ROWS, j=GRID, q=4, u=2)
+            for u in range(2):
+                places = x_sorted[u][:].rearrange("p j (c h r q) -> p c h j r q", c=2, h=ROW_HALVES, r=ROWS, q=4)
+                sorters[u](out=places[:, c, h], in_=words[:, u])
+            if part != parts[-1]:
+                keep_clock(unread, part, WARM_PER_PART)
+
+        x_grouped = operands.tile([P, HALVES * PASSES, 4 * COLS], BF16, name="x_grouped", align_bytes=64)
+        x_grouped_words = x_grouped[:].bitcast(F32).rearrange("p n (j m u) -> p n j m u", j=GRID, u=2)
+        x_codes = operands.tile([P, HALVES * PASSES, COLS], U32, name="x_codes", align_bytes=64)
+        x_scales = operands.tile([P, HALVES * PASSES, COLS], U8, name="x_scales", align_bytes=64)
+
+        def quantise(n, first, cols):
+            nc.vector.quantize_mx(
+                out=x_codes[:, n, first : first + cols].bitcast(FP8X4),
+                scales=x_scales[:, n, first : first + cols],
+                in_=x_grouped[:, n, 4 * first : 4 * (first + cols)],
+            )
+
+        def quantise_first_half(quarter):
+            for g in range(PASSES):
+                quantise(g, quarter * COLS // 4, COLS // 4)
+
+        banks = GRID // 2
+        for bank in range(banks):
+            x_turned = psum.tile([P, 2, 2, P], F32, name="x_turned", tag="bank")
+            for jj in range(2):
+                for u in range(2):
+                    nc.tensor.transpose(x_turned[:, jj, u, :], x_sorted[u][:, 2 * bank + jj, :], ident[:])
+            copy_out = nc.vector.tensor_copy if bank % 2 == 1 and bank != banks - 1 else nc.scalar.copy
+            for jj in range(2):
+                copy_out(
+                    out=x_grouped_words[:, :, 2 * bank + jj, :, :],
+                    in_=x_turned[:, jj].rearrange("p u (m n) -> p n m u", n=HALVES * PASSES),
+                )
+            if bank % 2 == 1 and bank >= 3:
+                quantise_first_half((bank - 3) // 2)
+        quantise_first_half(3)
+        unread_too = psum.tile([P, COLS], F32, name="unread_too", tag="bank")
+        keep_clock(unread_too, parts[-1], WARM_AFTER)
+
         kv = []
         left = []
         right = []
@@ -159,27 +210,8 @@ def tile_attentionconv_kernel(tc, x, W_qkv_words, W_qkv_scales, b_qkv, out):
                 nc.scalar.activation(
                     out=right[rh][:, GRID - 1, ch], in_=one_column, func=ACT.Identity, bias=right_outside[:, tile_col]
                 )
-
-        sort_words(1)
-
-        x_grouped = operands.tile([P, HALVES * PASSES, 4 * COLS], BF16, name="x_grouped", align_bytes=64)
-        x_grouped_words = x_grouped[:].bitcast(F32).rearrange("p n (j m u) -> p n j m u", j=GRID, u=2)
-        for bank in range(GRID // 2):
-            x_turned = psum.tile([P, 2, 2, P], F32, name="x_turned", tag="bank")
-            for jj in range(2):
-                for u in range(2):
-                    nc.tensor.transpose(x_turned[:, jj, u, :], x_sorted[:, 2 * bank + jj, u, :], ident[:])
-            copy_out = nc.vector.tensor_copy if bank % 2 == 0 else nc.scalar.copy
-            for jj in range(2):
-                copy_out(
-                    out=x_grouped_words[:, :, 2 * bank + jj, :, :],
-                    in_=x_turned[:, jj].rearrange("p u (m n) -> p n m u", n=HALVES * PASSES),
-                )
-
-        x_codes = operands.tile([P, HALVES * PASSES, COLS], U32, name="x_codes", align_bytes=64)
-        x_scales = operands.tile([P, HALVES * PASSES, COLS], U8, name="x_scales", align_bytes=64)
-        for n in range(HALVES * PASSES):
-            nc.vector.quantize_mx(out=x_codes[:, n, :].bitcast(FP8X4), scales=x_scales[:, n, :], in_=x_grouped[:, n, :])
+        for g in range(PASSES):
+            quantise(PASSES + g, 0, COLS)
 
         def project(proj, half, ch, rh):
             first = proj * D + (ch * ROW_HALVES + rh) * P

@@ -252,28 +252,27 @@ def tile_attentionconv_kernel(tc, x, W_qkv_words, W_qkv_scales, b_qkv, out):
 
         halves_of_j = ((0, GRID // 2), (GRID // 2, GRID))
 
-        def sum_columns(rh):
-            col_sum = work.tile([P, GRID, CHANNELS, GRID, PAIR], F32, name="col_sum")
-            for j0, j1 in halves_of_j:
+        def sum_columns_step(rh, col_sum, step):
+            j0, j1 = halves_of_j[step % 2]
+            if step < 2:
                 nc.vector.scalar_tensor_tensor(
                     out=col_sum[:, j0:j1], in0=kv[rh][:, j0:j1, :, 0:GRID, :], scalar=factor(PREV_R + rh),
                     in1=kv[rh][:, j0:j1, :, 1 : GRID + 1, :], op0=ALU.mult, op1=ALU.add,
                 )
-            for j0, j1 in halves_of_j:
+            else:
                 nc.vector.scalar_tensor_tensor(
                     out=col_sum[:, j0:j1], in0=kv[rh][:, j0:j1, :, 2 : GRID + 2, :], scalar=factor(NEXT_R + rh),
                     in1=col_sum[:, j0:j1], op0=ALU.mult, op1=ALU.add,
                 )
-            for j0, j1 in halves_of_j:
-                nc.gpsimd.tensor_scalar(
-                    out=left[rh][:, max(j0, 1) : j1], in0=col_sum[:, max(j0, 1) - 1 : j1 - 1],
-                    scalar1=factor(PREV_S), scalar2=0.0, op0=ALU.mult, op1=ALU.add,
-                )
-                nc.gpsimd.tensor_scalar(
-                    out=right[rh][:, j0 : min(j1, GRID - 1)], in0=col_sum[:, j0 + 1 : min(j1, GRID - 1) + 1],
-                    scalar1=factor(NEXT_S), scalar2=0.0, op0=ALU.mult, op1=ALU.add,
-                )
-            return col_sum
+
+        def weigh_left(rh, col_sum, part):
+            j0, j1 = halves_of_j[part]
+            nc.scalar.activation(
+                out=left[rh][:, max(j0, 1) : j1], in_=col_sum[:, max(j0, 1) - 1 : j1 - 1], func=ACT.Copy, scale=factor(PREV_S)
+            )
+
+        def weigh_right(rh, col_sum):
+            nc.vector.tensor_scalar_mul(out=right[rh][:, 0 : GRID - 1], in0=col_sum[:, 1:GRID], scalar1=factor(NEXT_S))
 
         out_rows = out.rearrange(
             "(e h) c (i a l) (j s) -> h a e (c i) l j s", e=PAIR, h=HALVES, i=GRID, a=ROW_HALVES, l=ROWS, s=PATCH
@@ -285,32 +284,47 @@ def tile_attentionconv_kernel(tc, x, W_qkv_words, W_qkv_scales, b_qkv, out):
         def by_pixel_row(turned):
             return turned[:].rearrange("p j (l s) -> p l j s", l=ROWS)
 
-        def finish(half, rh, q_sb, col_sum):
-            pixels = work.tile([P, ROWS, GRID, PATCH], F32, name="pixels")
-            for bank in range(GRID // PER_BANK):
-                js = slice(bank * PER_BANK, (bank + 1) * PER_BANK)
-                q_turned = psum.tile([P, PER_BANK, P], F32, name="q_turned", tag="bank")
-                sum_turned = psum.tile([P, PER_BANK, P], F32, name="sum_turned", tag="bank")
-                for jj in range(PER_BANK):
-                    nc.tensor.transpose(q_turned[:, jj, :], columns_of(q_sb, bank * PER_BANK + jj), ident[:])
-                for jj in range(PER_BANK):
-                    terms = (col_sum, left[rh], right[rh])
-                    for n, term in enumerate(terms):
-                        nc.tensor.matmul(
-                            sum_turned[:, jj, :], lhsT=columns_of(term, bank * PER_BANK + jj), rhs=ident[:],
-                            is_transpose=True, start=(n == 0), stop=(n == len(terms) - 1),
-                        )
-                nc.scalar.copy(out=pixels[:, :, js, :], in_=by_pixel_row(q_turned))
-                nc.vector.tensor_mul(out=pixels[:, :, js, :], in0=by_pixel_row(sum_turned), in1=pixels[:, :, js, :])
-                for pair in range(PAIR):
-                    nc.sync.dma_start(out=out_rows[half][rh][pair][:, :, js, :], in_=pixels[pair:P:PAIR, :, js, :])
+        def finish_bank(half, rh, q_sb, col_sum, pixels, bank):
+            js = slice(bank * PER_BANK, (bank + 1) * PER_BANK)
+            q_turned = psum.tile([P, PER_BANK, P], F32, name="q_turned", tag="bank")
+            sum_turned = psum.tile([P, PER_BANK, P], F32, name="sum_turned", tag="bank")
+            for jj in range(PER_BANK):
+                nc.tensor.transpose(q_turned[:, jj, :], columns_of(q_sb, bank * PER_BANK + jj), ident[:])
+            for jj in range(PER_BANK):
+                terms = (col_sum, left[rh], right[rh])
+                for n, term in enumerate(terms):
+                    nc.tensor.matmul(
+                        sum_turned[:, jj, :], lhsT=columns_of(term, bank * PER_BANK + jj), rhs=ident[:],
+                        is_transpose=True, start=(n == 0), stop=(n == len(terms) - 1),
+                    )
+            nc.scalar.copy(out=pixels[:, :, js, :], in_=by_pixel_row(q_turned))
+            nc.vector.tensor_mul(out=pixels[:, :, js, :], in0=by_pixel_row(sum_turned), in1=pixels[:, :, js, :])
+            for pair in range(PAIR):
+                nc.sync.dma_start(out=out_rows[half][rh][pair][:, :, js, :], in_=pixels[pair:P:PAIR, :, js, :])
 
         waiting = None
+
+        def last_group_bank(bank):
+            if waiting is not None:
+                finish_bank(*waiting, bank)
+
         for half in range(HALVES):
             for rh in range(ROW_HALVES):
                 keys_times_values(half, rh)
-                col_sum = sum_columns(rh)
-                if waiting is not None:
-                    finish(*waiting)
-                waiting = (half, rh, queries(half, rh), col_sum)
-        finish(*waiting)
+                q_sb = queries(half, rh)
+                col_sum = work.tile([P, GRID, CHANNELS, GRID, PAIR], F32, name="col_sum")
+                sum_columns_step(rh, col_sum, 0)
+                sum_columns_step(rh, col_sum, 1)
+                sum_columns_step(rh, col_sum, 2)
+                last_group_bank(0)
+                sum_columns_step(rh, col_sum, 3)
+                last_group_bank(1)
+                weigh_left(rh, col_sum, 0)
+                weigh_right(rh, col_sum)
+                last_group_bank(2)
+                weigh_left(rh, col_sum, 1)
+                last_group_bank(3)
+                pixels = work.tile([P, ROWS, GRID, PATCH], F32, name="pixels")
+                waiting = (half, rh, q_sb, col_sum, pixels)
+        for bank in range(GRID // PER_BANK):
+            last_group_bank(bank)

@@ -35,6 +35,8 @@ NEXT_S = 1
 PREV_R = 2
 NEXT_R = 4
 
+FIRST = 2
+DIRECT_BANK = 2
 WARM_PER_PART = 3
 WARM_AFTER = 5
 
@@ -195,13 +197,13 @@ def tile_attentionconv_kernel(tc, x, W_qkv_words, W_qkv_scales, b_qkv, out):
         left = []
         right = []
         for rh in range(ROW_HALVES):
-            kv.append(consts.tile([P, GRID, CHANNELS, GRID + 2, PAIR], F32, name="kv%d" % rh))
+            kv.append(consts.tile([P, GRID, CHANNELS, GRID + 4, PAIR], F32, name="kv%d" % rh))
             left.append(consts.tile([P, GRID, CHANNELS, GRID, PAIR], F32, name="left%d" % rh))
             right.append(consts.tile([P, GRID, CHANNELS, GRID, PAIR], F32, name="right%d" % rh))
             for ch in range(CHANNELS):
                 tile_col = slice(ch * ROW_HALVES + rh, ch * ROW_HALVES + rh + 1)
                 nc.vector.tensor_scalar_add(
-                    out=kv[rh][:, :, ch, 0 : GRID + 2 : GRID + 1, :],
+                    out=kv[rh][:, :, ch, FIRST - 1 : FIRST + GRID + 1 : GRID + 1, :],
                     in0=zeros[:].rearrange("p (j a e) -> p j a e", a=2, e=PAIR),
                     scalar1=kv_outside[:, tile_col],
                 )
@@ -228,27 +230,23 @@ def tile_attentionconv_kernel(tc, x, W_qkv_words, W_qkv_scales, b_qkv, out):
                 )
             return acc[:].rearrange("p (j i e) -> p j i e", j=GRID, e=PAIR)
 
-        def keys_times_values(half, rh):
-            for ch in range(CHANNELS):
-                k_acc = project(K, half, ch, rh)
-                v_acc = project(V, half, ch, rh)
-                k_sb = work.tile([P, GRID, GRID, PAIR], F32, name="k_sb", bufs=CHANNELS)
-                nc.scalar.activation(out=k_sb[:], in_=k_acc, func=ACT.Identity, bias=bias_of(K, ch, rh))
-                nc.vector.scalar_tensor_tensor(
-                    out=kv[rh][:, :, ch, 1 : GRID + 1, :],
-                    in0=v_acc,
-                    scalar=bias_of(V, ch, rh),
-                    in1=k_sb[:],
-                    op0=ALU.add,
-                    op1=ALU.mult,
-                )
+        def keys_times_values(half, rh, ch):
+            k_acc = project(K, half, ch, rh)
+            v_acc = project(V, half, ch, rh)
+            k_sb = work.tile([P, GRID, GRID, PAIR], F32, name="k_sb", bufs=CHANNELS)
+            nc.scalar.activation(out=k_sb[:], in_=k_acc, func=ACT.Identity, bias=bias_of(K, ch, rh))
+            nc.vector.scalar_tensor_tensor(
+                out=kv[rh][:, :, ch, FIRST : FIRST + GRID, :],
+                in0=v_acc,
+                scalar=bias_of(V, ch, rh),
+                in1=k_sb[:],
+                op0=ALU.add,
+                op1=ALU.mult,
+            )
 
-        def queries(half, rh):
-            q_sb = work.tile([P, GRID, CHANNELS, GRID, PAIR], F32, name="q_sb")
-            for ch in range(CHANNELS):
-                q_acc = project(Q, half, ch, rh)
-                nc.scalar.activation(out=q_sb[:, :, ch, :, :], in_=q_acc, func=ACT.Identity, bias=bias_of(Q, ch, rh))
-            return q_sb
+        def queries(half, rh, ch, q_sb):
+            q_acc = project(Q, half, ch, rh)
+            nc.scalar.activation(out=q_sb[:, :, ch, :, :], in_=q_acc, func=ACT.Identity, bias=bias_of(Q, ch, rh))
 
         halves_of_j = ((0, GRID // 2), (GRID // 2, GRID))
 
@@ -256,23 +254,45 @@ def tile_attentionconv_kernel(tc, x, W_qkv_words, W_qkv_scales, b_qkv, out):
             j0, j1 = halves_of_j[step % 2]
             if step < 2:
                 nc.vector.scalar_tensor_tensor(
-                    out=col_sum[:, j0:j1], in0=kv[rh][:, j0:j1, :, 0:GRID, :], scalar=factor(PREV_R + rh),
-                    in1=kv[rh][:, j0:j1, :, 1 : GRID + 1, :], op0=ALU.mult, op1=ALU.add,
+                    out=col_sum[:, j0:j1], in0=kv[rh][:, j0:j1, :, FIRST - 1 : FIRST - 1 + GRID, :], scalar=factor(PREV_R + rh),
+                    in1=kv[rh][:, j0:j1, :, FIRST : FIRST + GRID, :], op0=ALU.mult, op1=ALU.add,
                 )
             else:
                 nc.vector.scalar_tensor_tensor(
-                    out=col_sum[:, j0:j1], in0=kv[rh][:, j0:j1, :, 2 : GRID + 2, :], scalar=factor(NEXT_R + rh),
+                    out=col_sum[:, j0:j1], in0=kv[rh][:, j0:j1, :, FIRST + 1 : FIRST + 1 + GRID, :], scalar=factor(NEXT_R + rh),
                     in1=col_sum[:, j0:j1], op0=ALU.mult, op1=ALU.add,
                 )
 
+        direct_js = (DIRECT_BANK * PER_BANK, (DIRECT_BANK + 1) * PER_BANK)
+        added_js = ((0, direct_js[0]), (direct_js[1], GRID))
+
         def weigh_left(rh, col_sum, part):
-            j0, j1 = halves_of_j[part]
+            j0, j1 = added_js[part]
             nc.scalar.activation(
                 out=left[rh][:, max(j0, 1) : j1], in_=col_sum[:, max(j0, 1) - 1 : j1 - 1], func=ACT.Copy, scale=factor(PREV_S)
             )
 
-        def weigh_right(rh, col_sum):
-            nc.vector.tensor_scalar_mul(out=right[rh][:, 0 : GRID - 1], in0=col_sum[:, 1:GRID], scalar1=factor(NEXT_S))
+        def weigh_right(rh, col_sum, part):
+            j0, j1 = added_js[part]
+            nc.gpsimd.tensor_scalar(
+                out=right[rh][:, j0 : min(j1, GRID - 1)], in0=col_sum[:, j0 + 1 : min(j1, GRID - 1) + 1],
+                scalar1=factor(NEXT_S), scalar2=0.0, op0=ALU.mult, op1=ALU.add,
+            )
+
+        def direct_step(rh, q_sb, col_sum, direct, step):
+            j0, j1 = direct_js
+            if step == 0:
+                nc.vector.scalar_tensor_tensor(
+                    out=direct[:], in0=col_sum[:, j0 - 1 : j1 - 1], scalar=factor(PREV_S), in1=col_sum[:, j0:j1],
+                    op0=ALU.mult, op1=ALU.add,
+                )
+            elif step == 1:
+                nc.vector.scalar_tensor_tensor(
+                    out=direct[:], in0=col_sum[:, j0 + 1 : j1 + 1], scalar=factor(NEXT_S), in1=direct[:],
+                    op0=ALU.mult, op1=ALU.add,
+                )
+            else:
+                nc.vector.tensor_mul(out=direct[:], in0=direct[:], in1=q_sb[:, j0:j1])
 
         out_rows = out.rearrange(
             "(e h) c (i a l) (j s) -> h a e (c i) l j s", e=PAIR, h=HALVES, i=GRID, a=ROW_HALVES, l=ROWS, s=PATCH
@@ -284,25 +304,40 @@ def tile_attentionconv_kernel(tc, x, W_qkv_words, W_qkv_scales, b_qkv, out):
         def by_pixel_row(turned):
             return turned[:].rearrange("p j (l s) -> p l j s", l=ROWS)
 
-        def finish_bank(half, rh, q_sb, col_sum, pixels, bank):
+        def finish_bank(half, rh, q_sb, col_sum, direct, pixels, bank):
             js = slice(bank * PER_BANK, (bank + 1) * PER_BANK)
-            q_turned = psum.tile([P, PER_BANK, P], F32, name="q_turned", tag="bank")
-            sum_turned = psum.tile([P, PER_BANK, P], F32, name="sum_turned", tag="bank")
-            for jj in range(PER_BANK):
-                nc.tensor.transpose(q_turned[:, jj, :], columns_of(q_sb, bank * PER_BANK + jj), ident[:])
-            for jj in range(PER_BANK):
-                terms = (col_sum, left[rh], right[rh])
-                for n, term in enumerate(terms):
-                    nc.tensor.matmul(
-                        sum_turned[:, jj, :], lhsT=columns_of(term, bank * PER_BANK + jj), rhs=ident[:],
-                        is_transpose=True, start=(n == 0), stop=(n == len(terms) - 1),
-                    )
-            nc.scalar.copy(out=pixels[:, :, js, :], in_=by_pixel_row(q_turned))
-            nc.vector.tensor_mul(out=pixels[:, :, js, :], in0=by_pixel_row(sum_turned), in1=pixels[:, :, js, :])
+            if bank == DIRECT_BANK:
+                turned = psum.tile([P, PER_BANK, P], F32, name="turned", tag="bank")
+                for jj in range(PER_BANK):
+                    nc.tensor.transpose(turned[:, jj, :], columns_of(direct, jj), ident[:])
+                nc.scalar.copy(out=pixels[:, :, js, :], in_=by_pixel_row(turned))
+            else:
+                q_turned = psum.tile([P, PER_BANK, P], F32, name="q_turned", tag="bank")
+                sum_turned = psum.tile([P, PER_BANK, P], F32, name="sum_turned", tag="bank")
+                for jj in range(PER_BANK):
+                    nc.tensor.transpose(q_turned[:, jj, :], columns_of(q_sb, bank * PER_BANK + jj), ident[:])
+                for jj in range(PER_BANK):
+                    terms = (col_sum, left[rh], right[rh])
+                    for n, term in enumerate(terms):
+                        nc.tensor.matmul(
+                            sum_turned[:, jj, :], lhsT=columns_of(term, bank * PER_BANK + jj), rhs=ident[:],
+                            is_transpose=True, start=(n == 0), stop=(n == len(terms) - 1),
+                        )
+                nc.scalar.copy(out=pixels[:, :, js, :], in_=by_pixel_row(q_turned))
+                nc.vector.tensor_mul(out=pixels[:, :, js, :], in0=by_pixel_row(sum_turned), in1=pixels[:, :, js, :])
             for pair in range(PAIR):
                 nc.sync.dma_start(out=out_rows[half][rh][pair][:, :, js, :], in_=pixels[pair:P:PAIR, :, js, :])
 
+        DIRECT_STEPS = 3
         waiting = None
+
+        def last_group_gap_work(gap):
+            if waiting is not None:
+                half, rh, q_sb, col_sum, direct, pixels = waiting
+                if gap < DIRECT_STEPS:
+                    direct_step(rh, q_sb, col_sum, direct, gap)
+                if gap < len(added_js):
+                    weigh_left(rh, col_sum, gap)
 
         def last_group_bank(bank):
             if waiting is not None:
@@ -310,21 +345,27 @@ def tile_attentionconv_kernel(tc, x, W_qkv_words, W_qkv_scales, b_qkv, out):
 
         for half in range(HALVES):
             for rh in range(ROW_HALVES):
-                keys_times_values(half, rh)
-                q_sb = queries(half, rh)
+                for ch in range(CHANNELS):
+                    keys_times_values(half, rh, ch)
+                    last_group_gap_work(ch)
+                q_sb = work.tile([P, GRID, CHANNELS, GRID, PAIR], F32, name="q_sb")
+                for ch in range(CHANNELS):
+                    queries(half, rh, ch, q_sb)
                 col_sum = work.tile([P, GRID, CHANNELS, GRID, PAIR], F32, name="col_sum")
                 sum_columns_step(rh, col_sum, 0)
                 sum_columns_step(rh, col_sum, 1)
                 sum_columns_step(rh, col_sum, 2)
                 last_group_bank(0)
                 sum_columns_step(rh, col_sum, 3)
+                weigh_right(rh, col_sum, 0)
+                weigh_right(rh, col_sum, 1)
                 last_group_bank(1)
-                weigh_left(rh, col_sum, 0)
-                weigh_right(rh, col_sum)
                 last_group_bank(2)
-                weigh_left(rh, col_sum, 1)
                 last_group_bank(3)
+                direct = work.tile([P, PER_BANK, CHANNELS, GRID, PAIR], F32, name="direct")
                 pixels = work.tile([P, ROWS, GRID, PATCH], F32, name="pixels")
-                waiting = (half, rh, q_sb, col_sum, pixels)
+                waiting = (half, rh, q_sb, col_sum, direct, pixels)
+        for gap in range(CHANNELS):
+            last_group_gap_work(gap)
         for bank in range(GRID // PER_BANK):
             last_group_bank(bank)

@@ -38,7 +38,7 @@ NEXT_R = 4
 FIRST = 2
 DIRECT_BANK = 2
 WARM_PER_PART = 3
-WARM_AFTER = 5
+EARLY_CHANNELS = 2
 
 FLOPS = 2 * 4 * GRID * GRID * D * 3 * D
 
@@ -73,9 +73,9 @@ def tile_attentionconv_kernel(tc, x, W_qkv_words, W_qkv_scales, b_qkv, out):
                 in_=W_qkv_scales[:, 4 * quadrant : 4 * quadrant + 4, :].rearrange("g r n -> r g n").bitcast(I32),
             )
         w_words = operands.tile([P, PASSES, 2 * 3 * D], U8, name="w_words", align_bytes=64)
-        for proj in (K, V, Q):
+        for first_proj, last_proj in ((K, V), (Q, Q)):
             for g in range(PASSES):
-                cols = slice(2 * D * proj, 2 * D * (proj + 1))
+                cols = slice(2 * D * first_proj, 2 * D * (last_proj + 1))
                 nc.sync.dma_start(out=w_words[:, g, cols].bitcast(I32), in_=W_qkv_words[g, :, cols].bitcast(I32))
 
         ident = consts.tile([P, P], F32, name="ident")
@@ -190,8 +190,29 @@ def tile_attentionconv_kernel(tc, x, W_qkv_words, W_qkv_scales, b_qkv, out):
             if bank % 2 == 1 and bank >= 3:
                 quantise_first_half((bank - 3) // 2)
         quantise_first_half(3)
-        unread_too = psum.tile([P, COLS], F32, name="unread_too", tag="bank")
-        keep_clock(unread_too, parts[-1], WARM_AFTER)
+
+        def project_columns(acc, proj, half, ch, rh, first_col, cols):
+            first = proj * D + (ch * ROW_HALVES + rh) * P
+            for g in range(PASSES):
+                nc.tensor.matmul_mx(
+                    out=acc[:, first_col : first_col + cols],
+                    lhsT=w_words[:, g, 2 * first : 2 * (first + P)].bitcast(FP4X4),
+                    lhsT_scale=w_scales[:, g, first : first + P],
+                    rhs=x_codes[:, half * PASSES + g, first_col : first_col + cols].bitcast(FP8X4),
+                    rhs_scale=x_scales[:, half * PASSES + g, first_col : first_col + cols],
+                    start=(g == 0),
+                    stop=(g == PASSES - 1),
+                )
+
+        early = {}
+        for ch in range(EARLY_CHANNELS):
+            k_early = psum.tile([P, COLS], F32, name="k_early", tag="bank")
+            v_early = psum.tile([P, COLS], F32, name="v_early", tag="bank")
+            early[0, 0, ch] = (k_early, v_early)
+        for quarter in range(4):
+            for ch in range(EARLY_CHANNELS):
+                for proj, acc in zip((K, V), early[0, 0, ch]):
+                    project_columns(acc, proj, 0, ch, 0, quarter * COLS // 4, COLS // 4)
 
         kv = []
         left = []
@@ -215,29 +236,24 @@ def tile_attentionconv_kernel(tc, x, W_qkv_words, W_qkv_scales, b_qkv, out):
         for g in range(PASSES):
             quantise(PASSES + g, 0, COLS)
 
-        def project(proj, half, ch, rh):
-            first = proj * D + (ch * ROW_HALVES + rh) * P
-            acc = psum.tile([P, COLS], F32, name="acc", tag="bank")
-            for g in range(PASSES):
-                nc.tensor.matmul_mx(
-                    out=acc[:],
-                    lhsT=w_words[:, g, 2 * first : 2 * (first + P)].bitcast(FP4X4),
-                    lhsT_scale=w_scales[:, g, first : first + P],
-                    rhs=x_codes[:, half * PASSES + g, :].bitcast(FP8X4),
-                    rhs_scale=x_scales[:, half * PASSES + g, :],
-                    start=(g == 0),
-                    stop=(g == PASSES - 1),
-                )
+        def by_patch(acc):
             return acc[:].rearrange("p (j i e) -> p j i e", j=GRID, e=PAIR)
 
+        def project(proj, half, ch, rh):
+            acc = psum.tile([P, COLS], F32, name="acc", tag="bank")
+            project_columns(acc, proj, half, ch, rh, 0, COLS)
+            return acc
+
         def keys_times_values(half, rh, ch):
-            k_acc = project(K, half, ch, rh)
-            v_acc = project(V, half, ch, rh)
+            made = early.get((half, rh, ch))
+            if made is None:
+                made = (project(K, half, ch, rh), project(V, half, ch, rh))
+            k_acc, v_acc = made
             k_sb = work.tile([P, GRID, GRID, PAIR], F32, name="k_sb", bufs=CHANNELS)
-            nc.scalar.activation(out=k_sb[:], in_=k_acc, func=ACT.Identity, bias=bias_of(K, ch, rh))
+            nc.scalar.activation(out=k_sb[:], in_=by_patch(k_acc), func=ACT.Identity, bias=bias_of(K, ch, rh))
             nc.vector.scalar_tensor_tensor(
                 out=kv[rh][:, :, ch, FIRST : FIRST + GRID, :],
-                in0=v_acc,
+                in0=by_patch(v_acc),
                 scalar=bias_of(V, ch, rh),
                 in1=k_sb[:],
                 op0=ALU.add,
@@ -246,7 +262,7 @@ def tile_attentionconv_kernel(tc, x, W_qkv_words, W_qkv_scales, b_qkv, out):
 
         def queries(half, rh, ch, q_sb):
             q_acc = project(Q, half, ch, rh)
-            nc.scalar.activation(out=q_sb[:, :, ch, :, :], in_=q_acc, func=ACT.Identity, bias=bias_of(Q, ch, rh))
+            nc.scalar.activation(out=q_sb[:, :, ch, :, :], in_=by_patch(q_acc), func=ACT.Identity, bias=bias_of(Q, ch, rh))
 
         halves_of_j = ((0, GRID // 2), (GRID // 2, GRID))
 

@@ -67,15 +67,16 @@ def tile_attentionconv_kernel(tc, x, W_qkv_words, W_qkv_scales, b_qkv, out):
 
         w_scales = operands.tile([P, PASSES, 3 * D], U8, name="w_scales", align_bytes=64)
         nc.vector.memset(w_scales[:].bitcast(I32), 0)
-        for quadrant in range(4):
-            nc.sync.dma_start(
-                out=w_scales[32 * quadrant : 32 * quadrant + 4, :, :].bitcast(I32),
-                in_=W_qkv_scales[:, 4 * quadrant : 4 * quadrant + 4, :].rearrange("g r n -> r g n").bitcast(I32),
-            )
         w_words = operands.tile([P, PASSES, 2 * 3 * D], U8, name="w_words", align_bytes=64)
         for first_proj, last_proj in ((K, V), (Q, Q)):
+            cols = slice(D * first_proj, D * (last_proj + 1))
+            for quadrant in range(4):
+                nc.sync.dma_start(
+                    out=w_scales[32 * quadrant : 32 * quadrant + 4, :, cols].bitcast(I32),
+                    in_=W_qkv_scales[:, 4 * quadrant : 4 * quadrant + 4, cols].rearrange("g r n -> r g n").bitcast(I32),
+                )
+            cols = slice(2 * D * first_proj, 2 * D * (last_proj + 1))
             for g in range(PASSES):
-                cols = slice(2 * D * first_proj, 2 * D * (last_proj + 1))
                 nc.sync.dma_start(out=w_words[:, g, cols].bitcast(I32), in_=W_qkv_words[g, :, cols].bitcast(I32))
 
         ident = consts.tile([P, P], F32, name="ident")

@@ -52,18 +52,18 @@ def tile_attentionconv_kernel(tc, x, W_qkv_words, W_qkv_scales, b_qkv, out):
         work = ctx.enter_context(tc.tile_pool(name="work", bufs=2))
         psum = ctx.enter_context(tc.psum_pool(name="psum", bufs=8))
 
-        b_rows = consts.tile([P, P], BF16, name="b_rows")
-        nc.vector.memset(b_rows[:], 0.0)
-        b_tiles = b_qkv.rearrange("(t p) -> t p", p=P)
-        for rows in (slice(0, 2 * TILES), slice(2 * TILES, 3 * TILES)):
-            nc.sync.dma_start(out=b_rows[rows, :], in_=b_tiles[rows, :])
-
         x_rows = x.rearrange("b (g c) (i h r) w -> c h i b g (r w)", g=PASSES, c=2, i=GRID, h=ROW_HALVES, r=ROWS)
         parts = [(c, h) for c in range(2) for h in range(ROW_HALVES)]
         x_nat = {}
         for c, h in parts:
             x_nat[c, h] = operands.tile([P, ROWS * GRID * PATCH], BF16, name="x_nat%d%d" % (c, h))
             nc.sync.dma_start(out=x_nat[c, h][:], in_=x_rows[c][h])
+
+        b_rows = consts.tile([P, P], BF16, name="b_rows")
+        nc.vector.memset(b_rows[:], 0.0)
+        b_tiles = b_qkv.rearrange("(t p) -> t p", p=P)
+        for rows in (slice(0, 2 * TILES), slice(2 * TILES, 3 * TILES)):
+            nc.sync.dma_start(out=b_rows[rows, :], in_=b_tiles[rows, :])
 
         w_scales = operands.tile([P, PASSES, 3 * D], U8, name="w_scales", align_bytes=64)
         nc.vector.memset(w_scales[:].bitcast(I32), 0)
@@ -116,12 +116,67 @@ def tile_attentionconv_kernel(tc, x, W_qkv_words, W_qkv_scales, b_qkv, out):
         zeros = consts.tile([P, 2 * GRID * PAIR], F32, name="zeros")
         nc.vector.memset(zeros[:], 0.0)
 
+        x_sorted = [operands.tile([P, GRID, P], F32, name="x_sorted%d" % u) for u in range(2)]
+        sorters = (nc.vector.tensor_copy, nc.scalar.copy)
+
+        def keep_clock(product, part, times):
+            for n in range(times):
+                nc.tensor.matmul(product[:], lhsT=idle_w[:], rhs=x_nat[part][:, 0:COLS], start=True, stop=True)
+
+        unread = psum.tile([P, COLS], F32, name="unread", tag="bank")
+        for part in parts:
+            c, h = part
+            words = x_nat[part][:].bitcast(F32).rearrange("p (r j q u) -> p u j r q", r=ROWS, j=GRID, q=4, u=2)
+            places = [
+                x_sorted[u][:].rearrange("p j (c h r q) -> p c h j r q", c=2, h=ROW_HALVES, r=ROWS, q=4)[:, c, h] for u in range(2)
+            ]
+            if part != parts[-1]:
+                for u in range(2):
+                    sorters[u](out=places[u], in_=words[:, u])
+                keep_clock(unread, part, WARM_PER_PART)
+            else:
+                nc.vector.tensor_copy(out=places[0], in_=words[:, 0])
+                nc.scalar.copy(out=places[1][:, 0 : GRID // 2], in_=words[:, 1, 0 : GRID // 2])
+                nc.vector.tensor_copy(out=places[1][:, GRID // 2 : GRID], in_=words[:, 1, GRID // 2 : GRID])
+
         b_square = consts.tile([P, P], F32, name="b_square")
         nc.vector.tensor_copy(out=b_square[:], in_=b_rows[:])
-        b_turned = psum.tile([P, P], F32, name="b_turned", tag="bank")
-        nc.tensor.transpose(b_turned[:], b_square[:], ident[:])
         bias = consts.tile([P, 3 * TILES], F32, name="bias")
-        nc.vector.tensor_copy(out=bias[:], in_=b_turned[:, 0 : 3 * TILES])
+
+        x_grouped = operands.tile([P, HALVES * PASSES, 4 * COLS], BF16, name="x_grouped", align_bytes=64)
+        x_grouped_words = x_grouped[:].bitcast(F32).rearrange("p n (b k u) -> p n b k u", b=GRID // 2, u=2)
+        x_codes = operands.tile([P, HALVES * PASSES, COLS], U32, name="x_codes", align_bytes=64)
+        x_scales = operands.tile([P, HALVES * PASSES, COLS], U8, name="x_scales", align_bytes=64)
+
+        def quantise(n, first, cols):
+            nc.vector.quantize_mx(
+                out=x_codes[:, n, first : first + cols].bitcast(FP8X4),
+                scales=x_scales[:, n, first : first + cols],
+                in_=x_grouped[:, n, 4 * first : 4 * (first + cols)],
+            )
+
+        def quantise_first_half(quarter):
+            for g in range(PASSES):
+                quantise(g, quarter * COLS // 4, COLS // 4)
+
+        banks = GRID // 2
+        for bank in range(banks):
+            x_turned = psum.tile([P, 2, 2, P], F32, name="x_turned", tag="bank")
+            for jj in range(2):
+                for u in range(2):
+                    nc.tensor.transpose(x_turned[:, u, jj, :], x_sorted[u][:, 2 * bank + jj, :], ident[:])
+            copy_out = nc.vector.tensor_copy if bank % 2 == 1 and bank != banks - 1 else nc.scalar.copy
+            copy_out(
+                out=x_grouped_words[:, :, bank, :, :],
+                in_=x_turned[:].rearrange("p u jj (m n) -> p n (jj m) u", n=HALVES * PASSES),
+            )
+            if bank % 2 == 1 and bank >= 3:
+                quantise_first_half((bank - 3) // 2)
+            if bank == banks // 2 - 1:
+                b_turned = psum.tile([P, P], F32, name="b_turned", tag="bank")
+                nc.tensor.transpose(b_turned[:], b_square[:], ident[:])
+                nc.vector.tensor_copy(out=bias[:], in_=b_turned[:, 0 : 3 * TILES])
+        quantise_first_half(3)
 
         def bias_of(proj, ch, rh):
             col = proj * TILES + ch * ROW_HALVES + rh
@@ -143,54 +198,6 @@ def tile_attentionconv_kernel(tc, x, W_qkv_words, W_qkv_scales, b_qkv, out):
         nc.vector.tensor_scalar_mul(out=left_outside[:], in0=col_outside[:], scalar1=factor(PREV_S))
         nc.vector.tensor_scalar_mul(out=right_outside[:], in0=col_outside[:], scalar1=factor(NEXT_S))
 
-        x_sorted = [operands.tile([P, GRID, P], F32, name="x_sorted%d" % u) for u in range(2)]
-        sorters = (nc.vector.tensor_copy, nc.scalar.copy)
-
-        def keep_clock(product, part, times):
-            for n in range(times):
-                nc.tensor.matmul(product[:], lhsT=idle_w[:], rhs=x_nat[part][:, 0:COLS], start=True, stop=True)
-
-        unread = psum.tile([P, COLS], F32, name="unread", tag="bank")
-        for part in parts:
-            c, h = part
-            words = x_nat[part][:].bitcast(F32).rearrange("p (r j q u) -> p u j r q", r=ROWS, j=GRID, q=4, u=2)
-            for u in range(2):
-                places = x_sorted[u][:].rearrange("p j (c h r q) -> p c h j r q", c=2, h=ROW_HALVES, r=ROWS, q=4)
-                sorters[u](out=places[:, c, h], in_=words[:, u])
-            if part != parts[-1]:
-                keep_clock(unread, part, WARM_PER_PART)
-
-        x_grouped = operands.tile([P, HALVES * PASSES, 4 * COLS], BF16, name="x_grouped", align_bytes=64)
-        x_grouped_words = x_grouped[:].bitcast(F32).rearrange("p n (j m u) -> p n j m u", j=GRID, u=2)
-        x_codes = operands.tile([P, HALVES * PASSES, COLS], U32, name="x_codes", align_bytes=64)
-        x_scales = operands.tile([P, HALVES * PASSES, COLS], U8, name="x_scales", align_bytes=64)
-
-        def quantise(n, first, cols):
-            nc.vector.quantize_mx(
-                out=x_codes[:, n, first : first + cols].bitcast(FP8X4),
-                scales=x_scales[:, n, first : first + cols],
-                in_=x_grouped[:, n, 4 * first : 4 * (first + cols)],
-            )
-
-        def quantise_first_half(quarter):
-            for g in range(PASSES):
-                quantise(g, quarter * COLS // 4, COLS // 4)
-
-        banks = GRID // 2
-        for bank in range(banks):
-            x_turned = psum.tile([P, 2, 2, P], F32, name="x_turned", tag="bank")
-            for jj in range(2):
-                for u in range(2):
-                    nc.tensor.transpose(x_turned[:, jj, u, :], x_sorted[u][:, 2 * bank + jj, :], ident[:])
-            copy_out = nc.vector.tensor_copy if bank % 2 == 1 and bank != banks - 1 else nc.scalar.copy
-            for jj in range(2):
-                copy_out(
-                    out=x_grouped_words[:, :, 2 * bank + jj, :, :],
-                    in_=x_turned[:, jj].rearrange("p u (m n) -> p n m u", n=HALVES * PASSES),
-                )
-            if bank % 2 == 1 and bank >= 3:
-                quantise_first_half((bank - 3) // 2)
-        quantise_first_half(3)
 
         def project_columns(acc, proj, half, ch, rh, first_col, cols):
             first = proj * D + (ch * ROW_HALVES + rh) * P
@@ -283,14 +290,14 @@ def tile_attentionconv_kernel(tc, x, W_qkv_words, W_qkv_scales, b_qkv, out):
         direct_js = (DIRECT_BANK * PER_BANK, (DIRECT_BANK + 1) * PER_BANK)
         added_js = ((0, direct_js[0]), (direct_js[1], GRID))
 
-        def weigh_left(rh, col_sum, part):
-            j0, j1 = added_js[part]
+        def weigh_left(rh, col_sum, js):
+            j0, j1 = js
             nc.scalar.activation(
                 out=left[rh][:, max(j0, 1) : j1], in_=col_sum[:, max(j0, 1) - 1 : j1 - 1], func=ACT.Copy, scale=factor(PREV_S)
             )
 
-        def weigh_right(rh, col_sum, part):
-            j0, j1 = added_js[part]
+        def weigh_right(rh, col_sum, js):
+            j0, j1 = js
             nc.gpsimd.tensor_scalar(
                 out=right[rh][:, j0 : min(j1, GRID - 1)], in0=col_sum[:, j0 + 1 : min(j1, GRID - 1) + 1],
                 scalar1=factor(NEXT_S), scalar2=0.0, op0=ALU.mult, op1=ALU.add,
@@ -321,7 +328,13 @@ def tile_attentionconv_kernel(tc, x, W_qkv_words, W_qkv_scales, b_qkv, out):
         def by_pixel_row(turned):
             return turned[:].rearrange("p j (l s) -> p l j s", l=ROWS)
 
-        def finish_bank(half, rh, q_sb, col_sum, direct, pixels, bank):
+        def turn_queries(q_sb, bank):
+            q_turned = psum.tile([P, PER_BANK, P], F32, name="q_turned", tag="bank")
+            for jj in range(PER_BANK):
+                nc.tensor.transpose(q_turned[:, jj, :], columns_of(q_sb, bank * PER_BANK + jj), ident[:])
+            return q_turned
+
+        def finish_bank(half, rh, q_sb, col_sum, direct, pixels, bank, q_turned=None):
             js = slice(bank * PER_BANK, (bank + 1) * PER_BANK)
             if bank == DIRECT_BANK:
                 turned = psum.tile([P, PER_BANK, P], F32, name="turned", tag="bank")
@@ -329,10 +342,9 @@ def tile_attentionconv_kernel(tc, x, W_qkv_words, W_qkv_scales, b_qkv, out):
                     nc.tensor.transpose(turned[:, jj, :], columns_of(direct, jj), ident[:])
                 nc.scalar.copy(out=pixels[:, :, js, :], in_=by_pixel_row(turned))
             else:
-                q_turned = psum.tile([P, PER_BANK, P], F32, name="q_turned", tag="bank")
+                if q_turned is None:
+                    q_turned = turn_queries(q_sb, bank)
                 sum_turned = psum.tile([P, PER_BANK, P], F32, name="sum_turned", tag="bank")
-                for jj in range(PER_BANK):
-                    nc.tensor.transpose(q_turned[:, jj, :], columns_of(q_sb, bank * PER_BANK + jj), ident[:])
                 for jj in range(PER_BANK):
                     terms = (col_sum, left[rh], right[rh])
                     for n, term in enumerate(terms):
@@ -354,35 +366,44 @@ def tile_attentionconv_kernel(tc, x, W_qkv_words, W_qkv_scales, b_qkv, out):
                 if gap < DIRECT_STEPS:
                     direct_step(rh, q_sb, col_sum, direct, gap)
                 if gap < len(added_js):
-                    weigh_left(rh, col_sum, gap)
+                    weigh_left(rh, col_sum, added_js[gap])
 
         def last_group_bank(bank):
             if waiting is not None:
                 finish_bank(*waiting, bank)
 
-        for half in range(HALVES):
-            for rh in range(ROW_HALVES):
-                for ch in range(CHANNELS):
-                    keys_times_values(half, rh, ch)
-                    last_group_gap_work(ch)
-                q_sb = work.tile([P, GRID, CHANNELS, GRID, PAIR], F32, name="q_sb")
-                for ch in range(CHANNELS):
-                    queries(half, rh, ch, q_sb)
-                col_sum = work.tile([P, GRID, CHANNELS, GRID, PAIR], F32, name="col_sum")
-                sum_columns_step(rh, col_sum, 0)
-                sum_columns_step(rh, col_sum, 1)
-                sum_columns_step(rh, col_sum, 2)
-                last_group_bank(0)
-                sum_columns_step(rh, col_sum, 3)
-                weigh_right(rh, col_sum, 0)
-                weigh_right(rh, col_sum, 1)
-                last_group_bank(1)
-                last_group_bank(2)
-                last_group_bank(3)
-                direct = work.tile([P, PER_BANK, CHANNELS, GRID, PAIR], F32, name="direct")
-                pixels = work.tile([P, ROWS, GRID, PATCH], F32, name="pixels")
-                waiting = (half, rh, q_sb, col_sum, direct, pixels)
-        for gap in range(CHANNELS):
-            last_group_gap_work(gap)
-        for bank in range(GRID // PER_BANK):
-            last_group_bank(bank)
+        banks = range(GRID // PER_BANK)
+        added_banks = [bank for bank in banks if bank != DIRECT_BANK]
+        js_of_added_banks = [(bank * PER_BANK, (bank + 1) * PER_BANK) for bank in added_banks]
+        groups = [(half, rh) for half in range(HALVES) for rh in range(ROW_HALVES)]
+        for half, rh in groups:
+            for ch in range(CHANNELS):
+                keys_times_values(half, rh, ch)
+                last_group_gap_work(ch)
+            q_sb = work.tile([P, GRID, CHANNELS, GRID, PAIR], F32, name="q_sb")
+            for ch in range(CHANNELS):
+                queries(half, rh, ch, q_sb)
+            col_sum = work.tile([P, GRID, CHANNELS, GRID, PAIR], F32, name="col_sum")
+            sum_columns_step(rh, col_sum, 0)
+            sum_columns_step(rh, col_sum, 1)
+            sum_columns_step(rh, col_sum, 2)
+            last_group_bank(0)
+            sum_columns_step(rh, col_sum, 3)
+            for js in js_of_added_banks if (half, rh) == groups[-1] else added_js:
+                weigh_right(rh, col_sum, js)
+            last_group_bank(1)
+            last_group_bank(2)
+            last_group_bank(3)
+            direct = work.tile([P, PER_BANK, CHANNELS, GRID, PAIR], F32, name="direct")
+            pixels = work.tile([P, ROWS, GRID, PATCH], F32, name="pixels")
+            waiting = (half, rh, q_sb, col_sum, direct, pixels)
+        half, rh, q_sb, col_sum, direct, pixels = waiting
+        for js in js_of_added_banks:
+            weigh_left(rh, col_sum, js)
+        for step in range(DIRECT_STEPS):
+            direct_step(rh, q_sb, col_sum, direct, step)
+        turned_before = {}
+        for bank in added_banks:
+            turned_before[bank] = turn_queries(q_sb, bank)
+        for bank in banks:
+            finish_bank(*waiting, bank, turned_before.get(bank))

@@ -334,13 +334,16 @@ def tile_attentionconv_kernel(tc, x, W_qkv_words, W_qkv_scales, b_qkv, out):
                 nc.tensor.transpose(q_turned[:, jj, :], columns_of(q_sb, bank * PER_BANK + jj), ident[:])
             return q_turned
 
-        def finish_bank(half, rh, q_sb, col_sum, direct, pixels, bank, q_turned=None):
+        def store(half, rh, pixels, js):
+            for pair in range(PAIR):
+                nc.sync.dma_start(out=out_rows[half][rh][pair][:, :, js, :], in_=pixels[pair:P:PAIR, :, js, :])
+
+        def finish_bank(half, rh, q_sb, col_sum, direct, pixels, bank, q_turned=None, stored=True):
             js = slice(bank * PER_BANK, (bank + 1) * PER_BANK)
             if bank == DIRECT_BANK:
                 turned = psum.tile([P, PER_BANK, P], F32, name="turned", tag="bank")
                 for jj in range(PER_BANK):
                     nc.tensor.transpose(turned[:, jj, :], columns_of(direct, jj), ident[:])
-                nc.scalar.copy(out=pixels[:, :, js, :], in_=by_pixel_row(turned))
             else:
                 if q_turned is None:
                     q_turned = turn_queries(q_sb, bank)
@@ -353,9 +356,12 @@ def tile_attentionconv_kernel(tc, x, W_qkv_words, W_qkv_scales, b_qkv, out):
                             is_transpose=True, start=(n == 0), stop=(n == len(terms) - 1),
                         )
                 nc.scalar.copy(out=pixels[:, :, js, :], in_=by_pixel_row(q_turned))
+            if bank == DIRECT_BANK:
+                nc.scalar.copy(out=pixels[:, :, js, :], in_=by_pixel_row(turned))
+            else:
                 nc.vector.tensor_mul(out=pixels[:, :, js, :], in0=by_pixel_row(sum_turned), in1=pixels[:, :, js, :])
-            for pair in range(PAIR):
-                nc.sync.dma_start(out=out_rows[half][rh][pair][:, :, js, :], in_=pixels[pair:P:PAIR, :, js, :])
+            if stored:
+                store(half, rh, pixels, js)
 
         DIRECT_STEPS = 3
         waiting = None
@@ -391,8 +397,8 @@ def tile_attentionconv_kernel(tc, x, W_qkv_words, W_qkv_scales, b_qkv, out):
             sum_columns_step(rh, col_sum, 3)
             for js in js_of_added_banks if (half, rh) == groups[-1] else added_js:
                 weigh_right(rh, col_sum, js)
-            last_group_bank(1)
             last_group_bank(2)
+            last_group_bank(1)
             last_group_bank(3)
             direct = work.tile([P, PER_BANK, CHANNELS, GRID, PAIR], F32, name="direct")
             pixels = work.tile([P, ROWS, GRID, PATCH], F32, name="pixels")
@@ -400,10 +406,14 @@ def tile_attentionconv_kernel(tc, x, W_qkv_words, W_qkv_scales, b_qkv, out):
         half, rh, q_sb, col_sum, direct, pixels = waiting
         for js in js_of_added_banks:
             weigh_left(rh, col_sum, js)
-        for step in range(DIRECT_STEPS):
-            direct_step(rh, q_sb, col_sum, direct, step)
         turned_before = {}
         for bank in added_banks:
             turned_before[bank] = turn_queries(q_sb, bank)
-        for bank in banks:
-            finish_bank(*waiting, bank, turned_before.get(bank))
+        direct_step(rh, q_sb, col_sum, direct, 0)
+        direct_step(rh, q_sb, col_sum, direct, 1)
+        finish_bank(*waiting, added_banks[0], turned_before[added_banks[0]])
+        direct_step(rh, q_sb, col_sum, direct, 2)
+        finish_bank(*waiting, added_banks[1], turned_before[added_banks[1]])
+        finish_bank(*waiting, added_banks[2], turned_before[added_banks[2]], False)
+        finish_bank(*waiting, DIRECT_BANK, None, False)
+        store(half, rh, pixels, slice(DIRECT_BANK * PER_BANK, GRID))

@@ -385,7 +385,8 @@ def tile_attentionconv_kernel(tc, x, W_qkv_words, W_qkv_scales, b_qkv, out):
         for half, rh in groups:
             for ch in range(CHANNELS):
                 keys_times_values(half, rh, ch)
-                last_group_gap_work(ch)
+                if ch != CHANNELS - 2:
+                    last_group_gap_work(ch if ch < CHANNELS - 2 else CHANNELS - 2)
             q_sb = work.tile([P, GRID, CHANNELS, GRID, PAIR], F32, name="q_sb")
             for ch in range(CHANNELS):
                 queries(half, rh, ch, q_sb)

@@ -113,8 +113,11 @@ def tile_attentionconv_kernel(tc, x, W_qkv_words, W_qkv_scales, b_qkv, out):
         def factor(col):
             return factors[:, col : col + 1]
 
-        zeros = consts.tile([P, 2 * GRID * PAIR], F32, name="zeros")
-        nc.vector.memset(zeros[:], 0.0)
+        column_weight = consts.tile([P, ROW_HALVES], F32, name="column_weight")
+        nc.vector.scalar_tensor_tensor(
+            out=column_weight[:], in0=factors[:, PREV_R : PREV_R + ROW_HALVES], scalar=1.0,
+            in1=factors[:, NEXT_R : NEXT_R + ROW_HALVES], op0=ALU.add, op1=ALU.add,
+        )
 
         x_sorted = [operands.tile([P, GRID, P], F32, name="x_sorted%d" % u) for u in range(2)]
         sorters = (nc.vector.tensor_copy, nc.scalar.copy)
@@ -182,22 +185,19 @@ def tile_attentionconv_kernel(tc, x, W_qkv_words, W_qkv_scales, b_qkv, out):
             col = proj * TILES + ch * ROW_HALVES + rh
             return bias[:, col : col + 1]
 
+        def weigh_columns(out, in0, weight):
+            nc.gpsimd.tensor_scalar(out=out, in0=in0, scalar1=weight, scalar2=0.0, op0=ALU.mult, op1=ALU.add)
+
         kv_outside = consts.tile([P, TILES], F32, name="kv_outside")
-        nc.vector.tensor_mul(out=kv_outside[:], in0=bias[:, K * TILES : (K + 1) * TILES], in1=bias[:, V * TILES : (V + 1) * TILES])
+        nc.gpsimd.tensor_mul(out=kv_outside[:], in0=bias[:, K * TILES : (K + 1) * TILES], in1=bias[:, V * TILES : (V + 1) * TILES])
         col_outside = consts.tile([P, TILES], F32, name="col_outside")
         for rh in range(ROW_HALVES):
-            r_factors = consts.tile([P, 1], F32, name="r_factors%d" % rh)
-            nc.vector.tensor_add(out=r_factors[:], in0=factor(PREV_R + rh), in1=factor(NEXT_R + rh))
             of_rh = slice(rh, TILES, ROW_HALVES)
-            nc.vector.scalar_tensor_tensor(
-                out=col_outside[:, of_rh], in0=kv_outside[:, of_rh], scalar=r_factors[:], in1=kv_outside[:, of_rh],
-                op0=ALU.mult, op1=ALU.add,
-            )
+            weigh_columns(col_outside[:, of_rh], kv_outside[:, of_rh], column_weight[:, rh : rh + 1])
         left_outside = consts.tile([P, TILES], F32, name="left_outside")
         right_outside = consts.tile([P, TILES], F32, name="right_outside")
-        nc.vector.tensor_scalar_mul(out=left_outside[:], in0=col_outside[:], scalar1=factor(PREV_S))
-        nc.vector.tensor_scalar_mul(out=right_outside[:], in0=col_outside[:], scalar1=factor(NEXT_S))
-
+        weigh_columns(left_outside[:], col_outside[:], factor(PREV_S))
+        weigh_columns(right_outside[:], col_outside[:], factor(NEXT_S))
 
         def project_columns(acc, proj, half, ch, rh, first_col, cols):
             first = proj * D + (ch * ROW_HALVES + rh) * P
@@ -229,20 +229,21 @@ def tile_attentionconv_kernel(tc, x, W_qkv_words, W_qkv_scales, b_qkv, out):
             kv.append(consts.tile([P, GRID, CHANNELS, GRID + 4, PAIR], F32, name="kv%d" % rh))
             left.append(consts.tile([P, GRID, CHANNELS, GRID, PAIR], F32, name="left%d" % rh))
             right.append(consts.tile([P, GRID, CHANNELS, GRID, PAIR], F32, name="right%d" % rh))
-            for ch in range(CHANNELS):
-                tile_col = slice(ch * ROW_HALVES + rh, ch * ROW_HALVES + rh + 1)
-                nc.vector.tensor_scalar_add(
-                    out=kv[rh][:, :, ch, FIRST - 1 : FIRST + GRID + 1 : GRID + 1, :],
-                    in0=zeros[:].rearrange("p (j a e) -> p j a e", a=2, e=PAIR),
-                    scalar1=kv_outside[:, tile_col],
+
+        def write_kv_outside(rh):
+            for place in (FIRST - 1, FIRST + GRID):
+                nc.scalar.copy(
+                    out=kv[rh][:, :, :, place, :],
+                    in_=kv_outside[:, rh:TILES:ROW_HALVES].unsqueeze(1).unsqueeze(3).to_broadcast([P, GRID, CHANNELS, PAIR]),
                 )
-                one_column = zeros[:, 0 : GRID * PAIR].rearrange("p (i e) -> p i e", e=PAIR)
-                nc.scalar.activation(out=left[rh][:, 0, ch], in_=one_column, func=ACT.Identity, bias=left_outside[:, tile_col])
-                nc.scalar.activation(
-                    out=right[rh][:, GRID - 1, ch], in_=one_column, func=ACT.Identity, bias=right_outside[:, tile_col]
-                )
-        for g in range(PASSES):
-            quantise(PASSES + g, 0, COLS)
+
+        def write_columns_outside():
+            for rh in range(ROW_HALVES):
+                for side, j, outside in ((left, 0, left_outside), (right, GRID - 1, right_outside)):
+                    nc.scalar.copy(
+                        out=side[rh][:, j].rearrange("p c i e -> p c (i e)"),
+                        in_=outside[:, rh:TILES:ROW_HALVES].unsqueeze(2).to_broadcast([P, CHANNELS, GRID * PAIR]),
+                    )
 
         def by_patch(acc):
             return acc[:].rearrange("p (j i e) -> p j i e", j=GRID, e=PAIR)
@@ -367,7 +368,14 @@ def tile_attentionconv_kernel(tc, x, W_qkv_words, W_qkv_scales, b_qkv, out):
         waiting = None
 
         def last_group_gap_work(gap):
-            if waiting is not None:
+            if waiting is None:
+                if gap < PASSES:
+                    quantise(PASSES + gap, 0, COLS)
+                if gap < ROW_HALVES:
+                    write_kv_outside(gap)
+                else:
+                    write_columns_outside()
+            else:
                 half, rh, q_sb, col_sum, direct, pixels = waiting
                 if gap < DIRECT_STEPS:
                     direct_step(rh, q_sb, col_sum, direct, gap)
@@ -391,6 +399,8 @@ def tile_attentionconv_kernel(tc, x, W_qkv_words, W_qkv_scales, b_qkv, out):
             for ch in range(CHANNELS):
                 queries(half, rh, ch, q_sb)
             col_sum = work.tile([P, GRID, CHANNELS, GRID, PAIR], F32, name="col_sum")
+            direct = work.tile([P, PER_BANK, CHANNELS, GRID, PAIR], F32, name="direct")
+            pixels = work.tile([P, ROWS, GRID, PATCH], F32, name="pixels")
             sum_columns_step(rh, col_sum, 0)
             sum_columns_step(rh, col_sum, 1)
             sum_columns_step(rh, col_sum, 2)
@@ -400,9 +410,9 @@ def tile_attentionconv_kernel(tc, x, W_qkv_words, W_qkv_scales, b_qkv, out):
                 weigh_right(rh, col_sum, js)
             last_group_bank(2)
             last_group_bank(1)
+            if (half, rh) == groups[-1]:
+                direct_step(rh, q_sb, col_sum, direct, 0)
             last_group_bank(3)
-            direct = work.tile([P, PER_BANK, CHANNELS, GRID, PAIR], F32, name="direct")
-            pixels = work.tile([P, ROWS, GRID, PATCH], F32, name="pixels")
             waiting = (half, rh, q_sb, col_sum, direct, pixels)
         half, rh, q_sb, col_sum, direct, pixels = waiting
         for js in js_of_added_banks:
@@ -410,7 +420,6 @@ def tile_attentionconv_kernel(tc, x, W_qkv_words, W_qkv_scales, b_qkv, out):
         turned_before = {}
         for bank in added_banks:
             turned_before[bank] = turn_queries(q_sb, bank)
-        direct_step(rh, q_sb, col_sum, direct, 0)
         direct_step(rh, q_sb, col_sum, direct, 1)
         finish_bank(*waiting, added_banks[0], turned_before[added_banks[0]])
         direct_step(rh, q_sb, col_sum, direct, 2)

@@ -231,10 +231,10 @@ def tile_attentionconv_kernel(tc, x, W_qkv_words, W_qkv_scales, b_qkv, out):
             right.append(consts.tile([P, GRID, CHANNELS, GRID, PAIR], F32, name="right%d" % rh))
 
         def write_kv_outside(rh):
-            for place in (FIRST - 1, FIRST + GRID):
+            for places in (slice(0, FIRST), slice(FIRST + GRID, FIRST + GRID + FIRST)):
                 nc.scalar.copy(
-                    out=kv[rh][:, :, :, place, :],
-                    in_=kv_outside[:, rh:TILES:ROW_HALVES].unsqueeze(1).unsqueeze(3).to_broadcast([P, GRID, CHANNELS, PAIR]),
+                    out=kv[rh][:, :, :, places, :].rearrange("p j c a e -> p j c (a e)"),
+                    in_=kv_outside[:, rh:TILES:ROW_HALVES].unsqueeze(1).unsqueeze(3).to_broadcast([P, GRID, CHANNELS, FIRST * PAIR]),
                 )
 
         def write_columns_outside():
@@ -244,6 +244,11 @@ def tile_attentionconv_kernel(tc, x, W_qkv_words, W_qkv_scales, b_qkv, out):
                         out=side[rh][:, j].rearrange("p c i e -> p c (i e)"),
                         in_=outside[:, rh:TILES:ROW_HALVES].unsqueeze(2).to_broadcast([P, CHANNELS, GRID * PAIR]),
                     )
+
+        for g in range(PASSES):
+            quantise(PASSES + g, 0, COLS)
+        for rh in range(ROW_HALVES):
+            write_kv_outside(rh)
 
         def by_patch(acc):
             return acc[:].rearrange("p (j i e) -> p j i e", j=GRID, e=PAIR)
@@ -367,20 +372,15 @@ def tile_attentionconv_kernel(tc, x, W_qkv_words, W_qkv_scales, b_qkv, out):
         DIRECT_STEPS = 3
         waiting = None
 
-        def last_group_gap_work(gap):
-            if waiting is None:
-                if gap < PASSES:
-                    quantise(PASSES + gap, 0, COLS)
-                if gap < ROW_HALVES:
-                    write_kv_outside(gap)
-                else:
-                    write_columns_outside()
-            else:
+        left_pieces = ((0, PER_BANK), (PER_BANK, direct_js[0]), (direct_js[1], direct_js[1] + 2), (direct_js[1] + 2, GRID))
+        direct_step_behind = {0: 0, 1: 1, CHANNELS - 1: 2}
+
+        def last_group_gap_work(ch):
+            if waiting is not None:
                 half, rh, q_sb, col_sum, direct, pixels = waiting
-                if gap < DIRECT_STEPS:
-                    direct_step(rh, q_sb, col_sum, direct, gap)
-                if gap < len(added_js):
-                    weigh_left(rh, col_sum, added_js[gap])
+                weigh_left(rh, col_sum, left_pieces[ch])
+                if ch in direct_step_behind:
+                    direct_step(rh, q_sb, col_sum, direct, direct_step_behind[ch])
 
         def last_group_bank(bank):
             if waiting is not None:
@@ -393,11 +393,12 @@ def tile_attentionconv_kernel(tc, x, W_qkv_words, W_qkv_scales, b_qkv, out):
         for half, rh in groups:
             for ch in range(CHANNELS):
                 keys_times_values(half, rh, ch)
-                if ch != CHANNELS - 2:
-                    last_group_gap_work(ch if ch < CHANNELS - 2 else CHANNELS - 2)
+                last_group_gap_work(ch)
             q_sb = work.tile([P, GRID, CHANNELS, GRID, PAIR], F32, name="q_sb")
             for ch in range(CHANNELS):
                 queries(half, rh, ch, q_sb)
+            if waiting is None:
+                write_columns_outside()
             col_sum = work.tile([P, GRID, CHANNELS, GRID, PAIR], F32, name="col_sum")
             direct = work.tile([P, PER_BANK, CHANNELS, GRID, PAIR], F32, name="direct")
             pixels = work.tile([P, ROWS, GRID, PATCH], F32, name="pixels")

@@ -258,6 +258,8 @@ def tile_attentionconv_kernel(tc, x, W_qkv_words, W_qkv_scales, b_qkv, out):
             project_columns(acc, proj, half, ch, rh, 0, COLS)
             return acc
 
+        halves_of_j = ((0, GRID // 2), (GRID // 2, GRID))
+
         def keys_times_values(half, rh, ch):
             made = early.get((half, rh, ch))
             if made is None:
@@ -265,20 +267,20 @@ def tile_attentionconv_kernel(tc, x, W_qkv_words, W_qkv_scales, b_qkv, out):
             k_acc, v_acc = made
             k_sb = work.tile([P, GRID, GRID, PAIR], F32, name="k_sb", bufs=CHANNELS)
             nc.scalar.activation(out=k_sb[:], in_=by_patch(k_acc), func=ACT.Identity, bias=bias_of(K, ch, rh))
-            nc.vector.scalar_tensor_tensor(
-                out=kv[rh][:, :, ch, FIRST : FIRST + GRID, :],
-                in0=by_patch(v_acc),
-                scalar=bias_of(V, ch, rh),
-                in1=k_sb[:],
-                op0=ALU.add,
-                op1=ALU.mult,
-            )
+            pieces = halves_of_j if ch == CHANNELS - 1 else ((0, GRID),)
+            for j0, j1 in pieces:
+                nc.vector.scalar_tensor_tensor(
+                    out=kv[rh][:, j0:j1, ch, FIRST : FIRST + GRID, :],
+                    in0=by_patch(v_acc)[:, j0:j1],
+                    scalar=bias_of(V, ch, rh),
+                    in1=k_sb[:, j0:j1],
+                    op0=ALU.add,
+                    op1=ALU.mult,
+                )
 
         def queries(half, rh, ch, q_sb):
             q_acc = project(Q, half, ch, rh)
             nc.scalar.activation(out=q_sb[:, :, ch, :, :], in_=by_patch(q_acc), func=ACT.Identity, bias=bias_of(Q, ch, rh))
-
-        halves_of_j = ((0, GRID // 2), (GRID // 2, GRID))
 
         def sum_columns_step(rh, col_sum, step):
             j0, j1 = halves_of_j[step % 2]
@@ -373,14 +375,12 @@ def tile_attentionconv_kernel(tc, x, W_qkv_words, W_qkv_scales, b_qkv, out):
         waiting = None
 
         left_pieces = ((0, PER_BANK), (PER_BANK, direct_js[0]), (direct_js[1], direct_js[1] + 2), (direct_js[1] + 2, GRID))
-        direct_step_behind = {0: 0, 1: 1, CHANNELS - 1: 2}
-
         def last_group_gap_work(ch):
             if waiting is not None:
                 half, rh, q_sb, col_sum, direct, pixels = waiting
                 weigh_left(rh, col_sum, left_pieces[ch])
-                if ch in direct_step_behind:
-                    direct_step(rh, q_sb, col_sum, direct, direct_step_behind[ch])
+                if ch < DIRECT_STEPS:
+                    direct_step(rh, q_sb, col_sum, direct, ch)
 
         def last_group_bank(bank):
             if waiting is not None:

from contextlib import ExitStack

import concourse.mybir as mybir
from concourse.masks import make_identity

F32 = mybir.dt.float32
BF16 = mybir.dt.bfloat16
I32 = mybir.dt.int32
U32 = mybir.dt.uint32
U8 = mybir.dt.uint8
FP8X4 = mybir.dt.float8_e4m3fn_x4
FP4X4 = mybir.dt.float4_e2m1fn_x4
ALU = mybir.AluOpType
ACT = mybir.ActivationFunctionType

P = 128
GRID = 16
PATCH = 16
CHANNELS = 4
D = CHANNELS * PATCH * PATCH
PASSES = 2
HALVES = 2
PAIR = 2
COLS = GRID * GRID * PAIR
ROW_HALVES = 2
ROWS = PATCH // ROW_HALVES
TILES = D // P
Q = 0
K = 1
V = 2
PER_BANK = 4

PREV_S = 0
NEXT_S = 1
PREV_R = 2
NEXT_R = 4

FIRST = 2
DIRECT_BANK = 2
WARM_PER_PART = 3
EARLY_CHANNELS = 2

FLOPS = 2 * 4 * GRID * GRID * D * 3 * D


def tile_attentionconv_kernel(tc, x, W_qkv_words, W_qkv_scales, b_qkv, out):
    nc = tc.nc
    with ExitStack() as ctx:
        ctx.enter_context(tc.manual_schedule())
        consts = ctx.enter_context(tc.tile_pool(name="consts", bufs=1))
        operands = ctx.enter_context(tc.tile_pool(name="operands", bufs=1))
        work = ctx.enter_context(tc.tile_pool(name="work", bufs=2))
        psum = ctx.enter_context(tc.psum_pool(name="psum", bufs=8))

        x_rows = x.rearrange("b (g c) (i h r) w -> c h i b g (r w)", g=PASSES, c=2, i=GRID, h=ROW_HALVES, r=ROWS)
        parts = [(c, h) for c in range(2) for h in range(ROW_HALVES)]
        x_nat = {}
        for c, h in parts:
            x_nat[c, h] = operands.tile([P, ROWS * GRID * PATCH], BF16, name="x_nat%d%d" % (c, h))
            nc.sync.dma_start(out=x_nat[c, h][:], in_=x_rows[c][h])

        b_rows = consts.tile([P, P], BF16, name="b_rows")
        nc.vector.memset(b_rows[:], 0.0)
        b_tiles = b_qkv.rearrange("(t p) -> t p", p=P)
        for rows in (slice(0, 2 * TILES), slice(2 * TILES, 3 * TILES)):
            nc.sync.dma_start(out=b_rows[rows, :], in_=b_tiles[rows, :])

        w_scales = operands.tile([P, PASSES, 3 * D], U8, name="w_scales", align_bytes=64)
        nc.vector.memset(w_scales[:].bitcast(I32), 0)
        w_words = operands.tile([P, PASSES, 2 * 3 * D], U8, name="w_words", align_bytes=64)
        for first_proj, last_proj in ((K, V), (Q, Q)):
            cols = slice(D * first_proj, D * (last_proj + 1))
            for quadrant in range(4):
                nc.sync.dma_start(
                    out=w_scales[32 * quadrant : 32 * quadrant + 4, :, cols].bitcast(I32),
                    in_=W_qkv_scales[:, 4 * quadrant : 4 * quadrant + 4, cols].rearrange("g r n -> r g n").bitcast(I32),
                )
            cols = slice(2 * D * first_proj, 2 * D * (last_proj + 1))
            for g in range(PASSES):
                nc.sync.dma_start(out=w_words[:, g, cols].bitcast(I32), in_=W_qkv_words[g, :, cols].bitcast(I32))

        ident = consts.tile([P, P], F32, name="ident")
        part_idx = consts.tile([P, 1], I32, name="part_idx")
        nc.gpsimd.iota(part_idx[:], pattern=[[0, 1]], base=0, channel_multiplier=1)
        make_identity(nc, ident[:])
        idle_w = consts.tile([P, P], BF16, name="idle_w")
        nc.gpsimd.memset(idle_w[:], 0.0)

        s_int = consts.tile([P, 1], I32, name="s_int")
        r_int = consts.tile([P, 1], I32, name="r_int")
        nc.vector.tensor_single_scalar(out=s_int[:], in_=part_idx[:], scalar=PATCH - 1, op=ALU.bitwise_and)
        nc.vector.tensor_single_scalar(out=r_int[:], in_=part_idx[:], scalar=4, op=ALU.arith_shift_right)
        s_pos = consts.tile([P, 1], F32, name="s_pos")
        r_pos = consts.tile([P, 1], F32, name="r_pos")
        nc.vector.tensor_copy(out=s_pos[:], in_=s_int[:])
        nc.vector.tensor_copy(out=r_pos[:], in_=r_int[:])

        exponents = consts.tile([P, 6], F32, name="exponents")

        def exponent(col, pos, sign, offset):
            nc.vector.tensor_scalar(
                out=exponents[:, col : col + 1], in0=pos[:], scalar1=sign, scalar2=offset, op0=ALU.mult, op1=ALU.add
            )

        exponent(PREV_S, s_pos, 1.0, -15.0)
        exponent(NEXT_S, s_pos, -1.0, 0.0)
        for rh in range(ROW_HALVES):
            exponent(PREV_R + rh, r_pos, 1.0, ROWS * rh - 15.0)
            exponent(NEXT_R + rh, r_pos, -1.0, -1.0 * ROWS * rh)
        factors = consts.tile([P, 6], F32, name="factors")
        nc.scalar.activation(out=factors[:], in_=exponents[:], func=ACT.Exp, scale=1.0 / 8.0)

        def factor(col):
            return factors[:, col : col + 1]

        column_weight = consts.tile([P, ROW_HALVES], F32, name="column_weight")
        nc.vector.scalar_tensor_tensor(
            out=column_weight[:], in0=factors[:, PREV_R : PREV_R + ROW_HALVES], scalar=1.0,
            in1=factors[:, NEXT_R : NEXT_R + ROW_HALVES], op0=ALU.add, op1=ALU.add,
        )

        x_sorted = [operands.tile([P, GRID, P], F32, name="x_sorted%d" % u) for u in range(2)]
        sorters = (nc.vector.tensor_copy, nc.scalar.copy)

        def keep_clock(product, part, times):
            for n in range(times):
                nc.tensor.matmul(product[:], lhsT=idle_w[:], rhs=x_nat[part][:, 0:COLS], start=True, stop=True)

        unread = psum.tile([P, COLS], F32, name="unread", tag="bank")
        for part in parts:
            c, h = part
            words = x_nat[part][:].bitcast(F32).rearrange("p (r j q u) -> p u j r q", r=ROWS, j=GRID, q=4, u=2)
            places = [
                x_sorted[u][:].rearrange("p j (c h r q) -> p c h j r q", c=2, h=ROW_HALVES, r=ROWS, q=4)[:, c, h] for u in range(2)
            ]
            if part != parts[-1]:
                for u in range(2):
                    sorters[u](out=places[u], in_=words[:, u])
                keep_clock(unread, part, WARM_PER_PART)
            else:
                nc.vector.tensor_copy(out=places[0], in_=words[:, 0])
                nc.scalar.copy(out=places[1][:, 0 : GRID // 2], in_=words[:, 1, 0 : GRID // 2])
                nc.vector.tensor_copy(out=places[1][:, GRID // 2 : GRID], in_=words[:, 1, GRID // 2 : GRID])

        b_square = consts.tile([P, P], F32, name="b_square")
        nc.vector.tensor_copy(out=b_square[:], in_=b_rows[:])
        bias = consts.tile([P, 3 * TILES], F32, name="bias")

        x_grouped = operands.tile([P, HALVES * PASSES, 4 * COLS], BF16, name="x_grouped", align_bytes=64)
        x_grouped_words = x_grouped[:].bitcast(F32).rearrange("p n (b k u) -> p n b k u", b=GRID // 2, u=2)
        x_codes = operands.tile([P, HALVES * PASSES, COLS], U32, name="x_codes", align_bytes=64)
        x_scales = operands.tile([P, HALVES * PASSES, COLS], U8, name="x_scales", align_bytes=64)

        def quantise(n, first, cols):
            nc.vector.quantize_mx(
                out=x_codes[:, n, first : first + cols].bitcast(FP8X4),
                scales=x_scales[:, n, first : first + cols],
                in_=x_grouped[:, n, 4 * first : 4 * (first + cols)],
            )

        def quantise_first_half(quarter):
            for g in range(PASSES):
                quantise(g, quarter * COLS // 4, COLS // 4)

        banks = GRID // 2
        for bank in range(banks):
            x_turned = psum.tile([P, 2, 2, P], F32, name="x_turned", tag="bank")
            for jj in range(2):
                for u in range(2):
                    nc.tensor.transpose(x_turned[:, u, jj, :], x_sorted[u][:, 2 * bank + jj, :], ident[:])
            copy_out = nc.vector.tensor_copy if bank % 2 == 1 and bank != banks - 1 else nc.scalar.copy
            copy_out(
                out=x_grouped_words[:, :, bank, :, :],
                in_=x_turned[:].rearrange("p u jj (m n) -> p n (jj m) u", n=HALVES * PASSES),
            )
            if bank % 2 == 1 and bank >= 3:
                quantise_first_half((bank - 3) // 2)
            if bank == banks // 2 - 1:
                b_turned = psum.tile([P, P], F32, name="b_turned", tag="bank")
                nc.tensor.transpose(b_turned[:], b_square[:], ident[:])
                nc.vector.tensor_copy(out=bias[:], in_=b_turned[:, 0 : 3 * TILES])
        quantise_first_half(3)

        def bias_of(proj, ch, rh):
            col = proj * TILES + ch * ROW_HALVES + rh
            return bias[:, col : col + 1]

        def weigh_columns(out, in0, weight):
            nc.gpsimd.tensor_scalar(out=out, in0=in0, scalar1=weight, scalar2=0.0, op0=ALU.mult, op1=ALU.add)

        kv_outside = consts.tile([P, TILES], F32, name="kv_outside")
        nc.gpsimd.tensor_mul(out=kv_outside[:], in0=bias[:, K * TILES : (K + 1) * TILES], in1=bias[:, V * TILES : (V + 1) * TILES])
        col_outside = consts.tile([P, TILES], F32, name="col_outside")
        for rh in range(ROW_HALVES):
            of_rh = slice(rh, TILES, ROW_HALVES)
            weigh_columns(col_outside[:, of_rh], kv_outside[:, of_rh], column_weight[:, rh : rh + 1])
        left_outside = consts.tile([P, TILES], F32, name="left_outside")
        right_outside = consts.tile([P, TILES], F32, name="right_outside")
        weigh_columns(left_outside[:], col_outside[:], factor(PREV_S))
        weigh_columns(right_outside[:], col_outside[:], factor(NEXT_S))

        def project_columns(acc, proj, half, ch, rh, first_col, cols):
            first = proj * D + (ch * ROW_HALVES + rh) * P
            for g in range(PASSES):
                nc.tensor.matmul_mx(
                    out=acc[:, first_col : first_col + cols],
                    lhsT=w_words[:, g, 2 * first : 2 * (first + P)].bitcast(FP4X4),
                    lhsT_scale=w_scales[:, g, first : first + P],
                    rhs=x_codes[:, half * PASSES + g, first_col : first_col + cols].bitcast(FP8X4),
                    rhs_scale=x_scales[:, half * PASSES + g, first_col : first_col + cols],
                    start=(g == 0),
                    stop=(g == PASSES - 1),
                )

        early = {}
        for ch in range(EARLY_CHANNELS):
            k_early = psum.tile([P, COLS], F32, name="k_early", tag="bank")
            v_early = psum.tile([P, COLS], F32, name="v_early", tag="bank")
            early[0, 0, ch] = (k_early, v_early)
        for quarter in range(4):
            for ch in range(EARLY_CHANNELS):
                for proj, acc in zip((K, V), early[0, 0, ch]):
                    project_columns(acc, proj, 0, ch, 0, quarter * COLS // 4, COLS // 4)

        kv = []
        left = []
        right = []
        for rh in range(ROW_HALVES):
            kv.append(consts.tile([P, GRID, CHANNELS, GRID + 4, PAIR], F32, name="kv%d" % rh))
            left.append(consts.tile([P, GRID, CHANNELS, GRID, PAIR], F32, name="left%d" % rh))
            right.append(consts.tile([P, GRID, CHANNELS, GRID, PAIR], F32, name="right%d" % rh))

        def write_kv_outside(rh):
            for places in (slice(0, FIRST), slice(FIRST + GRID, FIRST + GRID + FIRST)):
                nc.scalar.copy(
                    out=kv[rh][:, :, :, places, :].rearrange("p j c a e -> p j c (a e)"),
                    in_=kv_outside[:, rh:TILES:ROW_HALVES].unsqueeze(1).unsqueeze(3).to_broadcast([P, GRID, CHANNELS, FIRST * PAIR]),
                )

        def write_columns_outside():
            for rh in range(ROW_HALVES):
                for side, j, outside in ((left, 0, left_outside), (right, GRID - 1, right_outside)):
                    nc.scalar.copy(
                        out=side[rh][:, j].rearrange("p c i e -> p c (i e)"),
                        in_=outside[:, rh:TILES:ROW_HALVES].unsqueeze(2).to_broadcast([P, CHANNELS, GRID * PAIR]),
                    )

        for g in range(PASSES):
            quantise(PASSES + g, 0, COLS)
        for rh in range(ROW_HALVES):
            write_kv_outside(rh)

        def by_patch(acc):
            return acc[:].rearrange("p (j i e) -> p j i e", j=GRID, e=PAIR)

        def project(proj, half, ch, rh):
            acc = psum.tile([P, COLS], F32, name="acc", tag="bank")
            project_columns(acc, proj, half, ch, rh, 0, COLS)
            return acc

        halves_of_j = ((0, GRID // 2), (GRID // 2, GRID))

        def keys_times_values(half, rh, ch):
            made = early.get((half, rh, ch))
            if made is None:
                made = (project(K, half, ch, rh), project(V, half, ch, rh))
            k_acc, v_acc = made
            k_sb = work.tile([P, GRID, GRID, PAIR], F32, name="k_sb", bufs=CHANNELS)
            nc.scalar.activation(out=k_sb[:], in_=by_patch(k_acc), func=ACT.Identity, bias=bias_of(K, ch, rh))
            pieces = halves_of_j if ch == CHANNELS - 1 else ((0, GRID),)
            for j0, j1 in pieces:
                nc.vector.scalar_tensor_tensor(
                    out=kv[rh][:, j0:j1, ch, FIRST : FIRST + GRID, :],
                    in0=by_patch(v_acc)[:, j0:j1],
                    scalar=bias_of(V, ch, rh),
                    in1=k_sb[:, j0:j1],
                    op0=ALU.add,
                    op1=ALU.mult,
                )

        def queries(half, rh, ch, q_sb):
            q_acc = project(Q, half, ch, rh)
            nc.scalar.activation(out=q_sb[:, :, ch, :, :], in_=by_patch(q_acc), func=ACT.Identity, bias=bias_of(Q, ch, rh))

        def sum_columns_step(rh, col_sum, step):
            j0, j1 = halves_of_j[step % 2]
            if step < 2:
                nc.vector.scalar_tensor_tensor(
                    out=col_sum[:, j0:j1], in0=kv[rh][:, j0:j1, :, FIRST - 1 : FIRST - 1 + GRID, :], scalar=factor(PREV_R + rh),
                    in1=kv[rh][:, j0:j1, :, FIRST : FIRST + GRID, :], op0=ALU.mult, op1=ALU.add,
                )
            else:
                nc.vector.scalar_tensor_tensor(
                    out=col_sum[:, j0:j1], in0=kv[rh][:, j0:j1, :, FIRST + 1 : FIRST + 1 + GRID, :], scalar=factor(NEXT_R + rh),
                    in1=col_sum[:, j0:j1], op0=ALU.mult, op1=ALU.add,
                )

        direct_js = (DIRECT_BANK * PER_BANK, (DIRECT_BANK + 1) * PER_BANK)
        added_js = ((0, direct_js[0]), (direct_js[1], GRID))

        def weigh_left(rh, col_sum, js):
            j0, j1 = js
            nc.scalar.activation(
                out=left[rh][:, max(j0, 1) : j1], in_=col_sum[:, max(j0, 1) - 1 : j1 - 1], func=ACT.Copy, scale=factor(PREV_S)
            )

        def weigh_right(rh, col_sum, js):
            j0, j1 = js
            nc.gpsimd.tensor_scalar(
                out=right[rh][:, j0 : min(j1, GRID - 1)], in0=col_sum[:, j0 + 1 : min(j1, GRID - 1) + 1],
                scalar1=factor(NEXT_S), scalar2=0.0, op0=ALU.mult, op1=ALU.add,
            )

        def direct_step(rh, q_sb, col_sum, direct, step):
            j0, j1 = direct_js
            if step == 0:
                nc.vector.scalar_tensor_tensor(
                    out=direct[:], in0=col_sum[:, j0 - 1 : j1 - 1], scalar=factor(PREV_S), in1=col_sum[:, j0:j1],
                    op0=ALU.mult, op1=ALU.add,
                )
            elif step == 1:
                nc.vector.scalar_tensor_tensor(
                    out=direct[:], in0=col_sum[:, j0 + 1 : j1 + 1], scalar=factor(NEXT_S), in1=direct[:],
                    op0=ALU.mult, op1=ALU.add,
                )
            else:
                nc.vector.tensor_mul(out=direct[:], in0=direct[:], in1=q_sb[:, j0:j1])

        out_rows = out.rearrange(
            "(e h) c (i a l) (j s) -> h a e (c i) l j s", e=PAIR, h=HALVES, i=GRID, a=ROW_HALVES, l=ROWS, s=PATCH
        )

        def columns_of(group_tile, j):
            return group_tile[:, j].rearrange("p c i e -> p (c i e)")

        def by_pixel_row(turned):
            return turned[:].rearrange("p j (l s) -> p l j s", l=ROWS)

        def turn_queries(q_sb, bank):
            q_turned = psum.tile([P, PER_BANK, P], F32, name="q_turned", tag="bank")
            for jj in range(PER_BANK):
                nc.tensor.transpose(q_turned[:, jj, :], columns_of(q_sb, bank * PER_BANK + jj), ident[:])
            return q_turned

        def store(half, rh, pixels, js):
            for pair in range(PAIR):
                nc.sync.dma_start(out=out_rows[half][rh][pair][:, :, js, :], in_=pixels[pair:P:PAIR, :, js, :])

        def finish_bank(half, rh, q_sb, col_sum, direct, pixels, bank, q_turned=None, stored=True):
            js = slice(bank * PER_BANK, (bank + 1) * PER_BANK)
            if bank == DIRECT_BANK:
                turned = psum.tile([P, PER_BANK, P], F32, name="turned", tag="bank")
                for jj in range(PER_BANK):
                    nc.tensor.transpose(turned[:, jj, :], columns_of(direct, jj), ident[:])
            else:
                if q_turned is None:
                    q_turned = turn_queries(q_sb, bank)
                sum_turned = psum.tile([P, PER_BANK, P], F32, name="sum_turned", tag="bank")
                for jj in range(PER_BANK):
                    terms = (col_sum, left[rh], right[rh])
                    for n, term in enumerate(terms):
                        nc.tensor.matmul(
                            sum_turned[:, jj, :], lhsT=columns_of(term, bank * PER_BANK + jj), rhs=ident[:],
                            is_transpose=True, start=(n == 0), stop=(n == len(terms) - 1),
                        )
                nc.scalar.copy(out=pixels[:, :, js, :], in_=by_pixel_row(q_turned))
            if bank == DIRECT_BANK:
                nc.scalar.copy(out=pixels[:, :, js, :], in_=by_pixel_row(turned))
            else:
                nc.vector.tensor_mul(out=pixels[:, :, js, :], in0=by_pixel_row(sum_turned), in1=pixels[:, :, js, :])
            if stored:
                store(half, rh, pixels, js)

        DIRECT_STEPS = 3
        waiting = None

        left_pieces = ((0, PER_BANK), (PER_BANK, direct_js[0]), (direct_js[1], direct_js[1] + 2), (direct_js[1] + 2, GRID))
        def last_group_gap_work(ch):
            if waiting is not None:
                half, rh, q_sb, col_sum, direct, pixels = waiting
                weigh_left(rh, col_sum, left_pieces[ch])
                if ch < DIRECT_STEPS:
                    direct_step(rh, q_sb, col_sum, direct, ch)

        def last_group_bank(bank):
            if waiting is not None:
                finish_bank(*waiting, bank)

        banks = range(GRID // PER_BANK)
        added_banks = [bank for bank in banks if bank != DIRECT_BANK]
        js_of_added_banks = [(bank * PER_BANK, (bank + 1) * PER_BANK) for bank in added_banks]
        groups = [(half, rh) for half in range(HALVES) for rh in range(ROW_HALVES)]
        for half, rh in groups:
            for ch in range(CHANNELS):
                keys_times_values(half, rh, ch)
                last_group_gap_work(ch)
            q_sb = work.tile([P, GRID, CHANNELS, GRID, PAIR], F32, name="q_sb")
            for ch in range(CHANNELS):
                queries(half, rh, ch, q_sb)
            if waiting is None:
                write_columns_outside()
            col_sum = work.tile([P, GRID, CHANNELS, GRID, PAIR], F32, name="col_sum")
            direct = work.tile([P, PER_BANK, CHANNELS, GRID, PAIR], F32, name="direct")
            pixels = work.tile([P, ROWS, GRID, PATCH], F32, name="pixels")
            sum_columns_step(rh, col_sum, 0)
            sum_columns_step(rh, col_sum, 1)
            sum_columns_step(rh, col_sum, 2)
            last_group_bank(0)
            sum_columns_step(rh, col_sum, 3)
            for js in js_of_added_banks if (half, rh) == groups[-1] else added_js:
                weigh_right(rh, col_sum, js)
            last_group_bank(2)
            last_group_bank(1)
            if (half, rh) == groups[-1]:
                direct_step(rh, q_sb, col_sum, direct, 0)
            last_group_bank(3)
            waiting = (half, rh, q_sb, col_sum, direct, pixels)
        half, rh, q_sb, col_sum, direct, pixels = waiting
        for js in js_of_added_banks:
            weigh_left(rh, col_sum, js)
        turned_before = {}
        for bank in added_banks:
            turned_before[bank] = turn_queries(q_sb, bank)
        direct_step(rh, q_sb, col_sum, direct, 1)
        finish_bank(*waiting, added_banks[0], turned_before[added_banks[0]])
        direct_step(rh, q_sb, col_sum, direct, 2)
        finish_bank(*waiting, added_banks[1], turned_before[added_banks[1]])
        finish_bank(*waiting, added_banks[2], turned_before[added_banks[2]], False)
        finish_bank(*waiting, DIRECT_BANK, None, False)
        store(half, rh, pixels, slice(DIRECT_BANK * PER_BANK, GRID))
